import numpy as np
import ml_dtypes


def mxq(x, axis, fmt="e4m3"):
    dtype, down = {"e4m3": (ml_dtypes.float8_e4m3fn, 7), "e5m2": (ml_dtypes.float8_e5m2, 14)}[fmt]
    v = np.moveaxis(np.asarray(x, np.float32).astype(ml_dtypes.bfloat16).astype(np.float64), axis, -1)
    blocks = v.reshape(v.shape[:-1] + (-1, 32))
    amax = np.abs(blocks).max(-1, keepdims=True)
    byte = np.maximum(np.where(amax > 0, np.frexp(amax)[1] - 1 + 127, 0) - down, 1)
    scale = np.exp2(byte - 127.0)
    codes = (blocks / scale).astype(np.float32).astype(dtype).astype(np.float64)
    return np.moveaxis((codes * scale).reshape(v.shape), -1, axis)


WIDE = False


def mx_kscale(k):
    if not WIDE:
        return np.ones(k)
    levels = np.array([10, -10, 5, -5, 0])
    a = np.random.permutation(np.resize(levels, k // 512 * 4)).reshape(k // 512, 4)
    idx = np.arange(k)
    return np.exp2(a[idx // 512, idx % 128 // 32])


BF16 = ml_dtypes.bfloat16


def bf(x):
    return np.asarray(x, np.float32).astype(BF16)


def f64(x):
    return np.asarray(x).astype(np.float64)


B, IN, H, G, GA, GB = 256, 1024, 512, 6, 4, 2
EPS = 1e-5


def layer_norm(v, g, b):
    mu = v.mean(-1, keepdims=True)
    var = np.square(v - mu).mean(-1, keepdims=True)
    return (v - mu) / np.sqrt(var + EPS) * g + b


def sigmoid(v):
    return 1.0 / (1.0 + np.exp(-v))


def setup_inputs():
    s = mx_kscale(IN)
    return {"x": bf(np.random.standard_normal((B, IN)) * s),
            "h": bf(np.random.standard_normal((B, H))),
            "c": bf(np.tanh(1.4 * np.random.standard_normal((B, H)))),
            "W_u": bf(np.random.standard_normal((H, H)) / np.sqrt(H)),
            "U_u": bf(np.random.standard_normal((H, IN)) / np.sqrt(IN) / s),
            "ln_gamma": bf(1.0 + 0.1 * np.random.standard_normal((GB, H))),
            "ln_beta": bf(0.2 * np.random.standard_normal((GB, H)))}


def reference(x, h, c, W_u, U_u, ln_gamma, ln_beta):
    g_uh, g_ux = f64(ln_gamma)
    b_uh, b_ux = f64(ln_beta)
    hf = f64(h)
    u = sigmoid(layer_norm(mxq(hf, 1, "e4m3") @ mxq(f64(W_u), 1, "e4m3").T, g_uh, b_uh)
                + layer_norm(mxq(f64(x), 1, "e4m3") @ mxq(f64(U_u), 1, "e4m3").T, g_ux, b_ux))
    return (1.0 - u) * hf + u * f64(c)

@@ -1,0 +1,179 @@
+from contextlib import ExitStack
+
+import concourse.mybir as mybir
+from concourse.masks import make_identity
+
+F32 = mybir.dt.float32
+BF16 = mybir.dt.bfloat16
+U32 = mybir.dt.uint32
+U8 = mybir.dt.uint8
+FP8X4 = mybir.dt.float8_e4m3fn_x4
+ALU = mybir.AluOpType
+ACT = mybir.ActivationFunctionType
+
+P = 128
+B, IN, H = 256, 1024, 512
+PACK = 4
+K_PASS = P * PACK
+ROW_TILES = B // P
+OUT_TILES = H // P
+EPS = 1e-5
+
+FLOPS = 2 * B * H * (H + IN)
+
+
+def load_rows(nc, pool, dram, tile_index, name):
+    rows = pool.tile([P, dram.shape[1]], BF16, name=name)
+    nc.sync.dma_start(out=rows[:], in_=dram[tile_index * P : (tile_index + 1) * P, :])
+    return rows
+
+
+def quantise_rows(nc, pools, ident, rows, copy_out, name):
+    k_len = rows.shape[1]
+    passes = k_len // K_PASS
+    row_words = rows[:].bitcast(F32)
+    flipped = pools["flipped"].tile([P, 2 * passes, P], F32, tag="flipped")
+    for v in range(2 * passes):
+        nc.tensor.transpose(flipped[:, v, :], row_words[:, v * P : (v + 1) * P], ident[:])
+    grouped = pools["stage"].tile([P, passes * P * PACK], BF16, align_bytes=64, name=name + "_grouped")
+    copy_out(
+        out=grouped[:].bitcast(F32).rearrange("p (g r u) -> p g r u", g=passes, u=2),
+        in_=flipped[:].rearrange("p (g u) r -> p g r u", u=2),
+    )
+    codes = pools["keep"].tile([P, passes * P], U32, align_bytes=64, name=name + "_codes")
+    scales = pools["keep"].tile([P, passes * P], U8, align_bytes=64, name=name + "_scales")
+    nc.vector.quantize_mx(out=codes[:].bitcast(FP8X4), scales=scales[:], in_=grouped[:])
+    return codes, scales
+
+
+def multiply(nc, acc, out_tile, acts, weights):
+    act_codes, act_scales = acts
+    w_codes, w_scales = weights
+    passes = w_codes.shape[1] // P
+    for g in range(passes):
+        cols = slice(g * P, (g + 1) * P)
+        nc.tensor.matmul_mx(
+            out=acc[:, out_tile * P : (out_tile + 1) * P],
+            lhsT=act_codes[:, cols].bitcast(FP8X4),
+            lhsT_scale=act_scales[:, cols],
+            rhs=w_codes[:, cols].bitcast(FP8X4),
+            rhs_scale=w_scales[:, cols],
+            start=(g == 0),
+            stop=(g == passes - 1),
+        )
+
+
+def add_layer_norm(nc, pools, acc, gamma, addend, neg_half, name):
+    stats = pools["small"].tile([P, 6], F32, name=name + "_stats")
+    nc.vector.bn_stats(out=stats[:], in_=acc[:])
+    mean_var = pools["small"].tile([P, 2], F32, name=name + "_mean_var")
+    nc.vector.bn_aggr(out=mean_var[:], in_=stats[:])
+    var_eps = pools["small"].tile([P, 1], F32, name=name + "_var_eps")
+    nc.vector.tensor_scalar_add(var_eps[:], mean_var[:, 1:2], EPS)
+    rstd = pools["small"].tile([P, 1], F32, name=name + "_rstd")
+    nc.gpsimd.tensor_tensor(out=rstd[:], in0=var_eps[:], in1=neg_half[:], op=ALU.pow)
+    centred = pools["work"].tile([P, H], F32, name=name + "_centred")
+    nc.vector.scalar_tensor_tensor(
+        out=centred[:], in0=acc[:], scalar=mean_var[:, 0:1], in1=gamma[:],
+        op0=ALU.subtract, op1=ALU.mult,
+    )
+    total = pools["work"].tile([P, H], F32, name=name + "_total")
+    nc.vector.scalar_tensor_tensor(
+        out=total[:], in0=centred[:], scalar=rstd[:], in1=addend[:],
+        op0=ALU.mult, op1=ALU.add,
+    )
+    return total
+
+
+def tile_layernormgrucell_pb_s_kernel(tc, x, h, c, W_u, U_u, ln_gamma, ln_beta, out):
+    nc = tc.nc
+    with ExitStack() as ctx:
+        pools = {
+            "const": ctx.enter_context(tc.tile_pool(name="const", bufs=1)),
+            "rows": ctx.enter_context(tc.tile_pool(name="rows", bufs=1)),
+            "stage": ctx.enter_context(tc.tile_pool(name="stage", bufs=1)),
+            "keep": ctx.enter_context(tc.tile_pool(name="keep", bufs=1)),
+            "small": ctx.enter_context(tc.tile_pool(name="small", bufs=1)),
+            "work": ctx.enter_context(tc.tile_pool(name="work", bufs=1)),
+            "flipped": ctx.enter_context(tc.psum_pool(name="flipped", bufs=4)),
+            "acc": ctx.enter_context(tc.psum_pool(name="acc", bufs=1)),
+        }
+        const = pools["const"]
+
+        ident = const.tile([P, P], F32)
+        make_identity(nc, ident[:])
+        neg_half = const.tile([P, 1], F32)
+        nc.vector.memset(neg_half[:], -0.5)
+        warm = const.tile([P, 1], F32)
+        nc.scalar.activation(out=warm[:], in_=neg_half[:], func=ACT.Sigmoid)
+
+        vec_rows = const.tile([P, 2, P], BF16)
+        nc.vector.memset(vec_rows[:], 0.0)
+        nc.sync.dma_start(out=vec_rows[0:8, 0, :], in_=ln_gamma.rearrange("l (q n) -> (l q) n", n=P))
+        nc.sync.dma_start(out=vec_rows[8:12, :, :], in_=ln_beta.rearrange("l (q n) -> q l n", n=P))
+        h_rows, c_rows = [], []
+        for i in range(ROW_TILES):
+            h_rows.append(load_rows(nc, pools["rows"], h, i, "h%d" % i))
+            c_rows.append(load_rows(nc, pools["rows"], c, i, "c%d" % i))
+        w_rows = [load_rows(nc, pools["rows"], W_u, j, "w%d" % j) for j in range(OUT_TILES)]
+        x_rows = [load_rows(nc, pools["rows"], x, i, "x%d" % i) for i in range(ROW_TILES)]
+        u_rows = [load_rows(nc, pools["rows"], U_u, j, "u%d" % j) for j in range(OUT_TILES)]
+
+        vec_f32 = const.tile([P, P], F32)
+        nc.vector.tensor_add(out=vec_f32[:], in0=vec_rows[:, 0, :], in1=vec_rows[:, 1, :])
+        vec_flipped = pools["flipped"].tile([P, OUT_TILES, P], F32, tag="flipped")
+        nc.tensor.transpose(vec_flipped[:, 0, :], vec_f32[:], ident[:])
+        vec_cols = const.tile([P, 3 * OUT_TILES], F32)
+        nc.scalar.copy(out=vec_cols[:], in_=vec_flipped[:, 0, 0 : 3 * OUT_TILES])
+        spread = []
+        for v in range(3):
+            spread_ps = pools["flipped"].tile([P, OUT_TILES, P], F32, tag="flipped")
+            for q in range(OUT_TILES):
+                col = v * OUT_TILES + q
+                nc.tensor.transpose(
+                    spread_ps[:, q, :], vec_cols[:, col : col + 1].to_broadcast([P, P]), ident[:]
+                )
+            spread_sb = const.tile([P, H], F32, name="spread%d" % v)
+            nc.scalar.copy(out=spread_sb[:], in_=spread_ps[:].rearrange("p q n -> p (q n)"))
+            spread.append(spread_sb)
+        gamma_h, gamma_x, beta_sum = spread
+
+        diff = []
+        for i in range(ROW_TILES):
+            d = pools["work"].tile([P, H], F32, name="diff%d" % i)
+            nc.vector.tensor_sub(out=d[:], in0=c_rows[i][:], in1=h_rows[i][:])
+            diff.append(d)
+
+        h_mx = [
+            quantise_rows(nc, pools, ident, h_rows[i], nc.vector.tensor_copy, "h%d" % i)
+            for i in range(ROW_TILES)
+        ]
+        acc_h = [pools["acc"].tile([P, H], F32, name="acc_h%d" % i) for i in range(ROW_TILES)]
+        for j in range(OUT_TILES):
+            w_mx = quantise_rows(nc, pools, ident, w_rows[j], nc.vector.tensor_copy, "w%d" % j)
+            for i in range(ROW_TILES):
+                multiply(nc, acc_h[i], j, h_mx[i], w_mx)
+        hidden_part = [
+            add_layer_norm(nc, pools, acc_h[i], gamma_h, beta_sum, neg_half, "hid%d" % i)
+            for i in range(ROW_TILES)
+        ]
+
+        x_mx = [
+            quantise_rows(nc, pools, ident, x_rows[i], nc.scalar.copy, "x%d" % i)
+            for i in range(ROW_TILES)
+        ]
+        acc_x = [pools["acc"].tile([P, H], F32, name="acc_x%d" % i) for i in range(ROW_TILES)]
+        for j in range(OUT_TILES):
+            u_mx = quantise_rows(nc, pools, ident, u_rows[j], nc.scalar.copy, "u%d" % j)
+            for i in range(ROW_TILES):
+                multiply(nc, acc_x[i], j, x_mx[i], u_mx)
+
+        for i in range(ROW_TILES):
+            logit = add_layer_norm(nc, pools, acc_x[i], gamma_x, hidden_part[i], neg_half, "inp%d" % i)
+            gate = pools["work"].tile([P, H], F32, name="gate%d" % i)
+            nc.scalar.activation(out=gate[:], in_=logit[:], func=ACT.Sigmoid)
+            step = pools["work"].tile([P, H], F32, name="step%d" % i)
+            nc.vector.tensor_mul(out=step[:], in0=gate[:], in1=diff[i][:])
+            result = pools["work"].tile([P, H], F32, name="result%d" % i)
+            nc.vector.tensor_add(out=result[:], in0=step[:], in1=h_rows[i][:])
+            nc.sync.dma_start(out=out[i * P : (i + 1) * P, :], in_=result[:])

@@ -17,72 +17,96 @@ PACK = 4
 K_PASS = P * PACK
 ROW_TILES = B // P
 OUT_TILES = H // P
+BLOCKS = 2
+W_UNITS = H // (BLOCKS * P)
+X_PASSES = IN // K_PASS
 EPS = 1e-5
 
 FLOPS = 2 * B * H * (H + IN)
 
 
-def load_rows(nc, pool, dram, tile_index, name):
-    rows = pool.tile([P, dram.shape[1]], BF16, name=name)
-    nc.sync.dma_start(out=rows[:], in_=dram[tile_index * P : (tile_index + 1) * P, :])
-    return rows
-
-
-def quantise_rows(nc, pools, ident, rows, copy_out, name):
-    k_len = rows.shape[1]
-    passes = k_len // K_PASS
-    row_words = rows[:].bitcast(F32)
-    flipped = pools["flipped"].tile([P, 2 * passes, P], F32, tag="flipped")
-    for v in range(2 * passes):
-        nc.tensor.transpose(flipped[:, v, :], row_words[:, v * P : (v + 1) * P], ident[:])
-    grouped = pools["stage"].tile([P, passes * P * PACK], BF16, align_bytes=64, name=name + "_grouped")
-    copy_out(
-        out=grouped[:].bitcast(F32).rearrange("p (g r u) -> p g r u", g=passes, u=2),
-        in_=flipped[:].rearrange("p (g u) r -> p g r u", u=2),
+def load_unit(nc, pool, dram, first_row, first_col, name):
+    unit = pool.tile([P, BLOCKS * K_PASS], BF16, name=name)
+    nc.sync.dma_start(
+        out=unit[:].rearrange("p (b k) -> p b k", b=BLOCKS),
+        in_=dram[first_row : first_row + BLOCKS * P, first_col : first_col + K_PASS].rearrange(
+            "(b p) k -> p b k", p=P
+        ),
     )
-    codes = pools["keep"].tile([P, passes * P], U32, align_bytes=64, name=name + "_codes")
-    scales = pools["keep"].tile([P, passes * P], U8, align_bytes=64, name=name + "_scales")
+    return unit
+
+
+def flip_unit(nc, pools, ident, unit, name):
+    unit_words = unit[:].bitcast(F32)
+    flipped = pools["flipped"].tile([P, 2 * BLOCKS, P], F32, tag="flipped")
+    for v in range(2 * BLOCKS):
+        nc.tensor.transpose(flipped[:, v, :], unit_words[:, v * P : (v + 1) * P], ident[:])
+    grouped = pools["stage"].tile([P, BLOCKS * P * PACK], BF16, align_bytes=64, name=name + "_grouped")
+    nc.scalar.copy(
+        out=grouped[:].bitcast(F32).rearrange("p (b r u) -> p b r u", b=BLOCKS, u=2),
+        in_=flipped[:].rearrange("p (b u) r -> p b r u", u=2),
+    )
+    return grouped
+
+
+def quantise_unit(nc, pools, grouped, name):
+    codes = pools["keep"].tile([P, BLOCKS * P], U32, align_bytes=64, name=name + "_codes")
+    scales = pools["keep"].tile([P, BLOCKS * P], U8, align_bytes=64, name=name + "_scales")
     nc.vector.quantize_mx(out=codes[:].bitcast(FP8X4), scales=scales[:], in_=grouped[:])
     return codes, scales
 
 
-def multiply(nc, acc, out_tile, acts, weights):
-    act_codes, act_scales = acts
-    w_codes, w_scales = weights
-    passes = w_codes.shape[1] // P
-    for g in range(passes):
-        cols = slice(g * P, (g + 1) * P)
-        nc.tensor.matmul_mx(
-            out=acc[:, out_tile * P : (out_tile + 1) * P],
-            lhsT=act_codes[:, cols].bitcast(FP8X4),
-            lhsT_scale=act_scales[:, cols],
-            rhs=w_codes[:, cols].bitcast(FP8X4),
-            rhs_scale=w_scales[:, cols],
-            start=(g == 0),
-            stop=(g == passes - 1),
-        )
+def mx_pass(nc, acc, weight_unit, acts, act_block, weights, start, stop):
+    a_cols = slice(act_block * P, (act_block + 1) * P)
+    nc.tensor.matmul_mx(
+        out=acc[:, weight_unit * BLOCKS * P : (weight_unit + 1) * BLOCKS * P],
+        lhsT=acts[0][:, a_cols].bitcast(FP8X4),
+        lhsT_scale=acts[1][:, a_cols],
+        rhs=weights[0][:].bitcast(FP8X4),
+        rhs_scale=weights[1][:],
+        start=start,
+        stop=stop,
+    )
 
 
 def add_layer_norm(nc, pools, acc, gamma, addend, neg_half, name):
-    stats = pools["small"].tile([P, 6], F32, name=name + "_stats")
-    nc.vector.bn_stats(out=stats[:], in_=acc[:])
-    mean_var = pools["small"].tile([P, 2], F32, name=name + "_mean_var")
-    nc.vector.bn_aggr(out=mean_var[:], in_=stats[:])
-    var_eps = pools["small"].tile([P, 1], F32, name=name + "_var_eps")
-    nc.vector.tensor_scalar_add(var_eps[:], mean_var[:, 1:2], EPS)
-    rstd = pools["small"].tile([P, 1], F32, name=name + "_rstd")
+    stats = pools["small"].tile([P, ROW_TILES, 6], F32, name=name + "_stats")
+    mean_var = pools["small"].tile([P, ROW_TILES, 2], F32, name=name + "_mean_var")
+    for i in range(ROW_TILES):
+        nc.vector.bn_stats(out=stats[:, i, :], in_=acc[i][:])
+    for i in range(ROW_TILES):
+        nc.vector.bn_aggr(out=mean_var[:, i, :], in_=stats[:, i, :])
+    var_eps = pools["small"].tile([P, ROW_TILES], F32, name=name + "_var_eps")
+    nc.vector.tensor_scalar_add(var_eps[:], mean_var[:, :, 1], EPS)
+    rstd = pools["small"].tile([P, ROW_TILES], F32, name=name + "_rstd")
     nc.gpsimd.tensor_tensor(out=rstd[:], in0=var_eps[:], in1=neg_half[:], op=ALU.pow)
-    centred = pools["work"].tile([P, H], F32, name=name + "_centred")
-    nc.vector.scalar_tensor_tensor(
-        out=centred[:], in0=acc[:], scalar=mean_var[:, 0:1], in1=gamma[:],
-        op0=ALU.subtract, op1=ALU.mult,
-    )
-    total = pools["work"].tile([P, H], F32, name=name + "_total")
-    nc.vector.scalar_tensor_tensor(
-        out=total[:], in0=centred[:], scalar=rstd[:], in1=addend[:],
-        op0=ALU.mult, op1=ALU.add,
-    )
+    centred = []
+    for i in range(ROW_TILES):
+        t = pools["work"].tile([P, H], F32, name="%s_centred%d" % (name, i))
+        nc.vector.scalar_tensor_tensor(
+            out=t[:], in0=acc[i][:], scalar=mean_var[:, i, 0:1], in1=gamma[:],
+            op0=ALU.subtract, op1=ALU.mult,
+        )
+        centred.append(t)
+    total = []
+    for i in range(ROW_TILES):
+        t = pools["work"].tile([P, H], F32, name="%s_total%d" % (name, i))
+        nc.vector.scalar_tensor_tensor(
+            out=t[:], in0=centred[i][:], scalar=rstd[:, i : i + 1], in1=addend[i][:],
+            op0=ALU.mult, op1=ALU.add,
+        )
+        total.append(t)
     return total
+
+
+def spread_vector(nc, pools, ident, vec_cols, v, name):
+    spread_ps = pools["flipped"].tile([P, OUT_TILES, P], F32, tag="flipped")
+    for q in range(OUT_TILES):
+        col = v * OUT_TILES + q
+        nc.tensor.transpose(spread_ps[:, q, :], vec_cols[:, col : col + 1].to_broadcast([P, P]), ident[:])
+    spread = pools["const"].tile([P, H], F32, name=name)
+    nc.scalar.copy(out=spread[:], in_=spread_ps[:].rearrange("p q n -> p (q n)"))
+    return spread
 
 
 def tile_layernormgrucell_pb_s_kernel(tc, x, h, c, W_u, U_u, ln_gamma, ln_beta, out):
@@ -100,24 +124,29 @@ def tile_layernormgrucell_pb_s_kernel(tc, x, h, c, W_u, U_u, ln_gamma, ln_beta, 
         }
         const = pools["const"]
 
-        ident = const.tile([P, P], F32)
-        make_identity(nc, ident[:])
-        neg_half = const.tile([P, 1], F32)
-        nc.vector.memset(neg_half[:], -0.5)
-        warm = const.tile([P, 1], F32)
-        nc.scalar.activation(out=warm[:], in_=neg_half[:], func=ACT.Sigmoid)
-
         vec_rows = const.tile([P, 2, P], BF16)
         nc.vector.memset(vec_rows[:], 0.0)
         nc.sync.dma_start(out=vec_rows[0:8, 0, :], in_=ln_gamma.rearrange("l (q n) -> (l q) n", n=P))
         nc.sync.dma_start(out=vec_rows[8:12, :, :], in_=ln_beta.rearrange("l (q n) -> q l n", n=P))
-        h_rows, c_rows = [], []
-        for i in range(ROW_TILES):
-            h_rows.append(load_rows(nc, pools["rows"], h, i, "h%d" % i))
-            c_rows.append(load_rows(nc, pools["rows"], c, i, "c%d" % i))
-        w_rows = [load_rows(nc, pools["rows"], W_u, j, "w%d" % j) for j in range(OUT_TILES)]
-        x_rows = [load_rows(nc, pools["rows"], x, i, "x%d" % i) for i in range(ROW_TILES)]
-        u_rows = [load_rows(nc, pools["rows"], U_u, j, "u%d" % j) for j in range(OUT_TILES)]
+
+        ident = const.tile([P, P], F32)
+        make_identity(nc, ident[:])
+        neg_half = const.tile([P, ROW_TILES], F32)
+        nc.vector.memset(neg_half[:], -0.5)
+        warm = const.tile([P, 1], F32)
+        nc.scalar.activation(out=warm[:], in_=neg_half[:, 0:1], func=ACT.Sigmoid)
+
+        rows = pools["rows"]
+        h_unit = load_unit(nc, rows, h, 0, 0, "h")
+        w_units = [load_unit(nc, rows, W_u, n * BLOCKS * P, 0, "w%d" % n) for n in range(W_UNITS)]
+        c_unit = load_unit(nc, rows, c, 0, 0, "c")
+        x_units = [load_unit(nc, rows, x, 0, g * K_PASS, "x%d" % g) for g in range(X_PASSES)]
+        u_units = [
+            [load_unit(nc, rows, U_u, n * BLOCKS * P, g * K_PASS, "u%d%d" % (n, g)) for g in range(X_PASSES)]
+            for n in range(W_UNITS)
+        ]
+
+        h_mx = quantise_unit(nc, pools, flip_unit(nc, pools, ident, h_unit, "h"), "h")
 
         vec_f32 = const.tile([P, P], F32)
         nc.vector.tensor_add(out=vec_f32[:], in0=vec_rows[:, 0, :], in1=vec_rows[:, 1, :])
@@ -125,55 +154,45 @@ def tile_layernormgrucell_pb_s_kernel(tc, x, h, c, W_u, U_u, ln_gamma, ln_beta, 
         nc.tensor.transpose(vec_flipped[:, 0, :], vec_f32[:], ident[:])
         vec_cols = const.tile([P, 3 * OUT_TILES], F32)
         nc.scalar.copy(out=vec_cols[:], in_=vec_flipped[:, 0, 0 : 3 * OUT_TILES])
-        spread = []
-        for v in range(3):
-            spread_ps = pools["flipped"].tile([P, OUT_TILES, P], F32, tag="flipped")
-            for q in range(OUT_TILES):
-                col = v * OUT_TILES + q
-                nc.tensor.transpose(
-                    spread_ps[:, q, :], vec_cols[:, col : col + 1].to_broadcast([P, P]), ident[:]
-                )
-            spread_sb = const.tile([P, H], F32, name="spread%d" % v)
-            nc.scalar.copy(out=spread_sb[:], in_=spread_ps[:].rearrange("p q n -> p (q n)"))
-            spread.append(spread_sb)
-        gamma_h, gamma_x, beta_sum = spread
 
-        diff = []
-        for i in range(ROW_TILES):
-            d = pools["work"].tile([P, H], F32, name="diff%d" % i)
-            nc.vector.tensor_sub(out=d[:], in0=c_rows[i][:], in1=h_rows[i][:])
-            diff.append(d)
-
-        h_mx = [
-            quantise_rows(nc, pools, ident, h_rows[i], nc.vector.tensor_copy, "h%d" % i)
-            for i in range(ROW_TILES)
+        w_mx = [
+            quantise_unit(nc, pools, flip_unit(nc, pools, ident, w_units[n], "w%d" % n), "w%d" % n)
+            for n in range(W_UNITS)
         ]
+        diff = pools["work"].tile([P, ROW_TILES * H], F32)
+        nc.vector.tensor_sub(out=diff[:], in0=c_unit[:], in1=h_unit[:])
+        gamma_h = spread_vector(nc, pools, ident, vec_cols, 0, "gamma_h")
+        beta_sum = spread_vector(nc, pools, ident, vec_cols, 2, "beta_sum")
         acc_h = [pools["acc"].tile([P, H], F32, name="acc_h%d" % i) for i in range(ROW_TILES)]
-        for j in range(OUT_TILES):
-            w_mx = quantise_rows(nc, pools, ident, w_rows[j], nc.vector.tensor_copy, "w%d" % j)
+        for n in range(W_UNITS):
             for i in range(ROW_TILES):
-                multiply(nc, acc_h[i], j, h_mx[i], w_mx)
-        hidden_part = [
-            add_layer_norm(nc, pools, acc_h[i], gamma_h, beta_sum, neg_half, "hid%d" % i)
-            for i in range(ROW_TILES)
-        ]
+                mx_pass(nc, acc_h[i], n, h_mx, i, w_mx[n], True, True)
 
-        x_mx = [
-            quantise_rows(nc, pools, ident, x_rows[i], nc.scalar.copy, "x%d" % i)
-            for i in range(ROW_TILES)
+        x_grouped = [flip_unit(nc, pools, ident, x_units[g], "x%d" % g) for g in range(X_PASSES)]
+        u_grouped = [
+            [flip_unit(nc, pools, ident, u_units[n][g], "u%d%d" % (n, g)) for g in range(X_PASSES)]
+            for n in range(W_UNITS)
         ]
+        hidden_part = add_layer_norm(nc, pools, acc_h, gamma_h, [beta_sum, beta_sum], neg_half, "hid")
+
+        x_mx = [quantise_unit(nc, pools, x_grouped[g], "x%d" % g) for g in range(X_PASSES)]
         acc_x = [pools["acc"].tile([P, H], F32, name="acc_x%d" % i) for i in range(ROW_TILES)]
-        for j in range(OUT_TILES):
-            u_mx = quantise_rows(nc, pools, ident, u_rows[j], nc.scalar.copy, "u%d" % j)
-            for i in range(ROW_TILES):
-                multiply(nc, acc_x[i], j, x_mx[i], u_mx)
+        for n in range(W_UNITS):
+            for g in range(X_PASSES):
+                u_mx = quantise_unit(nc, pools, u_grouped[n][g], "u%d%d" % (n, g))
+                for i in range(ROW_TILES):
+                    mx_pass(nc, acc_x[i], n, x_mx[g], i, u_mx, g == 0, g == X_PASSES - 1)
+        gamma_x = spread_vector(nc, pools, ident, vec_cols, 1, "gamma_x")
 
+        logit = add_layer_norm(nc, pools, acc_x, gamma_x, hidden_part, neg_half, "inp")
+        step = []
         for i in range(ROW_TILES):
-            logit = add_layer_norm(nc, pools, acc_x[i], gamma_x, hidden_part[i], neg_half, "inp%d" % i)
             gate = pools["work"].tile([P, H], F32, name="gate%d" % i)
-            nc.scalar.activation(out=gate[:], in_=logit[:], func=ACT.Sigmoid)
-            step = pools["work"].tile([P, H], F32, name="step%d" % i)
-            nc.vector.tensor_mul(out=step[:], in0=gate[:], in1=diff[i][:])
+            nc.scalar.activation(out=gate[:], in_=logit[i][:], func=ACT.Sigmoid)
+            t = pools["work"].tile([P, H], F32, name="step%d" % i)
+            nc.vector.tensor_mul(out=t[:], in0=gate[:], in1=diff[:, i * H : (i + 1) * H])
+            step.append(t)
+        for i in range(ROW_TILES):
             result = pools["work"].tile([P, H], F32, name="result%d" % i)
-            nc.vector.tensor_add(out=result[:], in0=step[:], in1=h_rows[i][:])
+            nc.vector.tensor_add(out=result[:], in0=step[i][:], in1=h_unit[:, i * H : (i + 1) * H])
             nc.sync.dma_start(out=out[i * P : (i + 1) * P, :], in_=result[:])

@@ -173,7 +173,6 @@ def tile_layernormgrucell_pb_s_kernel(tc, x, h, c, W_u, U_u, ln_gamma, ln_beta, 
             [flip_unit(nc, pools, ident, u_units[n][g], "u%d%d" % (n, g)) for g in range(X_PASSES)]
             for n in range(W_UNITS)
         ]
-        hidden_part = add_layer_norm(nc, pools, acc_h, gamma_h, [beta_sum, beta_sum], neg_half, "hid")
 
         x_mx = [quantise_unit(nc, pools, x_grouped[g], "x%d" % g) for g in range(X_PASSES)]
         acc_x = [pools["acc"].tile([P, H], F32, name="acc_x%d" % i) for i in range(ROW_TILES)]
@@ -182,6 +181,7 @@ def tile_layernormgrucell_pb_s_kernel(tc, x, h, c, W_u, U_u, ln_gamma, ln_beta, 
                 u_mx = quantise_unit(nc, pools, u_grouped[n][g], "u%d%d" % (n, g))
                 for i in range(ROW_TILES):
                     mx_pass(nc, acc_x[i], n, x_mx[g], i, u_mx, g == 0, g == X_PASSES - 1)
+        hidden_part = add_layer_norm(nc, pools, acc_h, gamma_h, [beta_sum, beta_sum], neg_half, "hid")
         gamma_x = spread_vector(nc, pools, ident, vec_cols, 1, "gamma_x")
 
         logit = add_layer_norm(nc, pools, acc_x, gamma_x, hidden_part, neg_half, "inp")

@@ -70,32 +70,24 @@ def mx_pass(nc, acc, weight_unit, acts, act_block, weights, start, stop):
 
 
 def add_layer_norm(nc, pools, acc, gamma, addend, neg_half, name):
-    stats = pools["small"].tile([P, ROW_TILES, 6], F32, name=name + "_stats")
-    mean_var = pools["small"].tile([P, ROW_TILES, 2], F32, name=name + "_mean_var")
-    for i in range(ROW_TILES):
-        nc.vector.bn_stats(out=stats[:, i, :], in_=acc[i][:])
-    for i in range(ROW_TILES):
-        nc.vector.bn_aggr(out=mean_var[:, i, :], in_=stats[:, i, :])
-    var_eps = pools["small"].tile([P, ROW_TILES], F32, name=name + "_var_eps")
-    nc.vector.tensor_scalar_add(var_eps[:], mean_var[:, :, 1], EPS)
-    rstd = pools["small"].tile([P, ROW_TILES], F32, name=name + "_rstd")
+    stats = pools["small"].tile([P, 6], F32, name=name + "_stats")
+    nc.vector.bn_stats(out=stats[:], in_=acc[:])
+    mean_var = pools["small"].tile([P, 2], F32, name=name + "_mean_var")
+    nc.vector.bn_aggr(out=mean_var[:], in_=stats[:])
+    var_eps = pools["small"].tile([P, 1], F32, name=name + "_var_eps")
+    nc.vector.tensor_scalar_add(var_eps[:], mean_var[:, 1:2], EPS)
+    rstd = pools["small"].tile([P, 1], F32, name=name + "_rstd")
     nc.gpsimd.tensor_tensor(out=rstd[:], in0=var_eps[:], in1=neg_half[:], op=ALU.pow)
-    centred = []
-    for i in range(ROW_TILES):
-        t = pools["work"].tile([P, H], F32, name="%s_centred%d" % (name, i))
-        nc.vector.scalar_tensor_tensor(
-            out=t[:], in0=acc[i][:], scalar=mean_var[:, i, 0:1], in1=gamma[:],
-            op0=ALU.subtract, op1=ALU.mult,
-        )
-        centred.append(t)
-    total = []
-    for i in range(ROW_TILES):
-        t = pools["work"].tile([P, H], F32, name="%s_total%d" % (name, i))
-        nc.vector.scalar_tensor_tensor(
-            out=t[:], in0=centred[i][:], scalar=rstd[:, i : i + 1], in1=addend[i][:],
-            op0=ALU.mult, op1=ALU.add,
-        )
-        total.append(t)
+    centred = pools["work"].tile([P, H], F32, name=name + "_centred")
+    nc.vector.scalar_tensor_tensor(
+        out=centred[:], in0=acc[:], scalar=mean_var[:, 0:1], in1=gamma[:],
+        op0=ALU.subtract, op1=ALU.mult,
+    )
+    total = pools["work"].tile([P, H], F32, name=name + "_total")
+    nc.vector.scalar_tensor_tensor(
+        out=total[:], in0=centred[:], scalar=rstd[:], in1=addend[:],
+        op0=ALU.mult, op1=ALU.add,
+    )
     return total
 
 
@@ -131,10 +123,10 @@ def tile_layernormgrucell_pb_s_kernel(tc, x, h, c, W_u, U_u, ln_gamma, ln_beta, 
 
         ident = const.tile([P, P], F32)
         make_identity(nc, ident[:])
-        neg_half = const.tile([P, ROW_TILES], F32)
+        neg_half = const.tile([P, 1], F32)
         nc.vector.memset(neg_half[:], -0.5)
         warm = const.tile([P, 1], F32)
-        nc.scalar.activation(out=warm[:], in_=neg_half[:, 0:1], func=ACT.Sigmoid)
+        nc.scalar.activation(out=warm[:], in_=neg_half[:], func=ACT.Sigmoid)
 
         rows = pools["rows"]
         h_unit = load_unit(nc, rows, h, 0, 0, "h")
@@ -181,18 +173,17 @@ def tile_layernormgrucell_pb_s_kernel(tc, x, h, c, W_u, U_u, ln_gamma, ln_beta, 
                 u_mx = quantise_unit(nc, pools, u_grouped[n][g], "u%d%d" % (n, g))
                 for i in range(ROW_TILES):
                     mx_pass(nc, acc_x[i], n, x_mx[g], i, u_mx, g == 0, g == X_PASSES - 1)
-        hidden_part = add_layer_norm(nc, pools, acc_h, gamma_h, [beta_sum, beta_sum], neg_half, "hid")
+        hidden_part = [
+            add_layer_norm(nc, pools, acc_h[i], gamma_h, beta_sum, neg_half, "hid%d" % i) for i in range(ROW_TILES)
+        ]
         gamma_x = spread_vector(nc, pools, ident, vec_cols, 1, "gamma_x")
 
-        logit = add_layer_norm(nc, pools, acc_x, gamma_x, hidden_part, neg_half, "inp")
-        step = []
         for i in range(ROW_TILES):
+            logit = add_layer_norm(nc, pools, acc_x[i], gamma_x, hidden_part[i], neg_half, "inp%d" % i)
             gate = pools["work"].tile([P, H], F32, name="gate%d" % i)
-            nc.scalar.activation(out=gate[:], in_=logit[i][:], func=ACT.Sigmoid)
-            t = pools["work"].tile([P, H], F32, name="step%d" % i)
-            nc.vector.tensor_mul(out=t[:], in0=gate[:], in1=diff[:, i * H : (i + 1) * H])
-            step.append(t)
-        for i in range(ROW_TILES):
+            nc.scalar.activation(out=gate[:], in_=logit[:], func=ACT.Sigmoid)
+            step = pools["work"].tile([P, H], F32, name="step%d" % i)
+            nc.vector.tensor_mul(out=step[:], in0=gate[:], in1=diff[:, i * H : (i + 1) * H])
             result = pools["work"].tile([P, H], F32, name="result%d" % i)
-            nc.vector.tensor_add(out=result[:], in0=step[i][:], in1=h_unit[:, i * H : (i + 1) * H])
+            nc.vector.tensor_add(out=result[:], in0=step[:], in1=h_unit[:, i * H : (i + 1) * H])
             nc.sync.dma_start(out=out[i * P : (i + 1) * P, :], in_=result[:])

@@ -25,22 +25,11 @@ EPS = 1e-5
 FLOPS = 2 * B * H * (H + IN)
 
 
-def load_unit(nc, pool, dram, first_row, first_col, name):
-    unit = pool.tile([P, BLOCKS * K_PASS], BF16, name=name)
-    nc.sync.dma_start(
-        out=unit[:].rearrange("p (b k) -> p b k", b=BLOCKS),
-        in_=dram[first_row : first_row + BLOCKS * P, first_col : first_col + K_PASS].rearrange(
-            "(b p) k -> p b k", p=P
-        ),
-    )
-    return unit
-
-
-def flip_unit(nc, pools, ident, unit, name):
-    unit_words = unit[:].bitcast(F32)
+def flip(nc, pools, ident, blocks, name):
     flipped = pools["flipped"].tile([P, 2 * BLOCKS, P], F32, tag="flipped")
-    for v in range(2 * BLOCKS):
-        nc.tensor.transpose(flipped[:, v, :], unit_words[:, v * P : (v + 1) * P], ident[:])
+    for b in range(BLOCKS):
+        for u in range(2):
+            nc.tensor.transpose(flipped[:, 2 * b + u, :], blocks[b][:, u * P : (u + 1) * P], ident[:])
     grouped = pools["stage"].tile([P, BLOCKS * P * PACK], BF16, align_bytes=64, name=name + "_grouped")
     nc.scalar.copy(
         out=grouped[:].bitcast(F32).rearrange("p (b r u) -> p b r u", b=BLOCKS, u=2),
@@ -49,19 +38,23 @@ def flip_unit(nc, pools, ident, unit, name):
     return grouped
 
 
-def quantise_unit(nc, pools, grouped, name):
-    codes = pools["keep"].tile([P, BLOCKS * P], U32, align_bytes=64, name=name + "_codes")
-    scales = pools["keep"].tile([P, BLOCKS * P], U8, align_bytes=64, name=name + "_scales")
-    nc.vector.quantize_mx(out=codes[:].bitcast(FP8X4), scales=scales[:], in_=grouped[:])
+def mx_tile(pools, width, name):
+    codes = pools["keep"].tile([P, width], U32, align_bytes=64, name=name + "_codes")
+    scales = pools["keep"].tile([P, width], U8, align_bytes=64, name=name + "_scales")
     return codes, scales
 
 
-def mx_pass(nc, acc, weight_unit, acts, act_block, weights, start, stop):
-    a_cols = slice(act_block * P, (act_block + 1) * P)
+def quantise(nc, grouped, mx, first):
+    cols = slice(first, first + BLOCKS * P)
+    nc.vector.quantize_mx(out=mx[0][:, cols].bitcast(FP8X4), scales=mx[1][:, cols], in_=grouped[:])
+
+
+def mx_pass(nc, acc, acts, block, weights, start, stop):
+    cols = slice(block * P, (block + 1) * P)
     nc.tensor.matmul_mx(
-        out=acc[:, weight_unit * BLOCKS * P : (weight_unit + 1) * BLOCKS * P],
-        lhsT=acts[0][:, a_cols].bitcast(FP8X4),
-        lhsT_scale=acts[1][:, a_cols],
+        out=acc[:],
+        lhsT=acts[0][:, cols].bitcast(FP8X4),
+        lhsT_scale=acts[1][:, cols],
         rhs=weights[0][:].bitcast(FP8X4),
         rhs_scale=weights[1][:],
         start=start,
@@ -129,16 +122,38 @@ def tile_layernormgrucell_pb_s_kernel(tc, x, h, c, W_u, U_u, ln_gamma, ln_beta, 
         nc.scalar.activation(out=warm[:], in_=neg_half[:], func=ACT.Sigmoid)
 
         rows = pools["rows"]
-        h_unit = load_unit(nc, rows, h, 0, 0, "h")
-        w_units = [load_unit(nc, rows, W_u, n * BLOCKS * P, 0, "w%d" % n) for n in range(W_UNITS)]
-        c_unit = load_unit(nc, rows, c, 0, 0, "c")
-        x_units = [load_unit(nc, rows, x, 0, g * K_PASS, "x%d" % g) for g in range(X_PASSES)]
-        u_units = [
-            [load_unit(nc, rows, U_u, n * BLOCKS * P, g * K_PASS, "u%d%d" % (n, g)) for g in range(X_PASSES)]
-            for n in range(W_UNITS)
-        ]
+        h_rows = rows.tile([P, ROW_TILES, H], BF16)
+        nc.sync.dma_start(out=h_rows[:], in_=h.rearrange("(p i) k -> p i k", i=ROW_TILES))
+        c_rows = rows.tile([P, ROW_TILES, H], BF16)
+        nc.sync.dma_start(out=c_rows[:], in_=c.rearrange("(p i) k -> p i k", i=ROW_TILES))
+        w_rows = []
+        for n in range(W_UNITS):
+            w = rows.tile([P, BLOCKS, H], BF16, name="w%d" % n)
+            nc.sync.dma_start(
+                out=w[:],
+                in_=W_u[n * BLOCKS * P : (n + 1) * BLOCKS * P, :].rearrange("(b p) k -> p b k", p=P),
+            )
+            w_rows.append(w)
+        u_rows = []
+        for n in range(W_UNITS):
+            u = rows.tile([P, BLOCKS, IN], BF16, name="u%d" % n)
+            nc.sync.dma_start(
+                out=u[:],
+                in_=U_u[n * BLOCKS * P : (n + 1) * BLOCKS * P, :].rearrange("(b p) k -> p b k", p=P),
+            )
+            u_rows.append(u)
+        x_rows = []
+        x_tiles = x.rearrange("(p i) k -> i p k", i=ROW_TILES)
+        for i in range(ROW_TILES):
+            xt = rows.tile([P, IN], BF16, name="x%d" % i)
+            nc.sync.dma_start(out=xt[:], in_=x_tiles[i])
+            x_rows.append(xt)
 
-        h_mx = quantise_unit(nc, pools, flip_unit(nc, pools, ident, h_unit, "h"), "h")
+        h_mx = mx_tile(pools, ROW_TILES * P, "h")
+        h_grouped = flip(nc, pools, ident, [h_rows[:, i, :].bitcast(F32) for i in range(ROW_TILES)], "h")
+        quantise(nc, h_grouped, h_mx, 0)
+        diff = pools["work"].tile([P, ROW_TILES, H], F32)
+        nc.vector.tensor_sub(out=diff[:], in0=c_rows[:], in1=h_rows[:])
 
         vec_f32 = const.tile([P, P], F32)
         nc.vector.tensor_add(out=vec_f32[:], in0=vec_rows[:, 0, :], in1=vec_rows[:, 1, :])
@@ -147,43 +162,48 @@ def tile_layernormgrucell_pb_s_kernel(tc, x, h, c, W_u, U_u, ln_gamma, ln_beta, 
         vec_cols = const.tile([P, 3 * OUT_TILES], F32)
         nc.scalar.copy(out=vec_cols[:], in_=vec_flipped[:, 0, 0 : 3 * OUT_TILES])
 
-        w_mx = [
-            quantise_unit(nc, pools, flip_unit(nc, pools, ident, w_units[n], "w%d" % n), "w%d" % n)
-            for n in range(W_UNITS)
-        ]
-        diff = pools["work"].tile([P, ROW_TILES * H], F32)
-        nc.vector.tensor_sub(out=diff[:], in0=c_unit[:], in1=h_unit[:])
+        w_mx = mx_tile(pools, H, "w")
+        for n in range(W_UNITS):
+            grouped = flip(nc, pools, ident, [w_rows[n][:, b, :].bitcast(F32) for b in range(BLOCKS)], "w%d" % n)
+            quantise(nc, grouped, w_mx, n * BLOCKS * P)
         gamma_h = spread_vector(nc, pools, ident, vec_cols, 0, "gamma_h")
         beta_sum = spread_vector(nc, pools, ident, vec_cols, 2, "beta_sum")
         acc_h = [pools["acc"].tile([P, H], F32, name="acc_h%d" % i) for i in range(ROW_TILES)]
-        for n in range(W_UNITS):
-            for i in range(ROW_TILES):
-                mx_pass(nc, acc_h[i], n, h_mx, i, w_mx[n], True, True)
+        for i in range(ROW_TILES):
+            mx_pass(nc, acc_h[i], h_mx, i, w_mx, True, True)
 
-        x_grouped = [flip_unit(nc, pools, ident, x_units[g], "x%d" % g) for g in range(X_PASSES)]
-        u_grouped = [
-            [flip_unit(nc, pools, ident, u_units[n][g], "u%d%d" % (n, g)) for g in range(X_PASSES)]
-            for n in range(W_UNITS)
-        ]
-
-        x_mx = [quantise_unit(nc, pools, x_grouped[g], "x%d" % g) for g in range(X_PASSES)]
-        acc_x = [pools["acc"].tile([P, H], F32, name="acc_x%d" % i) for i in range(ROW_TILES)]
+        u_mx = [mx_tile(pools, H, "u%d" % g) for g in range(X_PASSES)]
         for n in range(W_UNITS):
+            u_words = [u_rows[n][:, b, :].bitcast(F32) for b in range(BLOCKS)]
             for g in range(X_PASSES):
-                u_mx = quantise_unit(nc, pools, u_grouped[n][g], "u%d%d" % (n, g))
-                for i in range(ROW_TILES):
-                    mx_pass(nc, acc_x[i], n, x_mx[g], i, u_mx, g == 0, g == X_PASSES - 1)
+                blocks = [words[:, g * 2 * P : (g + 1) * 2 * P] for words in u_words]
+                grouped = flip(nc, pools, ident, blocks, "u%d%d" % (n, g))
+                quantise(nc, grouped, u_mx[g], n * BLOCKS * P)
+        gamma_x = spread_vector(nc, pools, ident, vec_cols, 1, "gamma_x")
+
         hidden_part = [
             add_layer_norm(nc, pools, acc_h[i], gamma_h, beta_sum, neg_half, "hid%d" % i) for i in range(ROW_TILES)
         ]
-        gamma_x = spread_vector(nc, pools, ident, vec_cols, 1, "gamma_x")
 
+        acc_x = []
+        for i in range(ROW_TILES):
+            x_words = x_rows[i][:].bitcast(F32)
+            blocks = [x_words[:, g * 2 * P : (g + 1) * 2 * P] for g in range(X_PASSES)]
+            grouped = flip(nc, pools, ident, blocks, "x%d" % i)
+            x_mx = mx_tile(pools, X_PASSES * P, "x%d" % i)
+            quantise(nc, grouped, x_mx, 0)
+            acc = pools["acc"].tile([P, H], F32, name="acc_x%d" % i)
+            for g in range(X_PASSES):
+                mx_pass(nc, acc, x_mx, g, u_mx[g], g == 0, g == X_PASSES - 1)
+            acc_x.append(acc)
+
+        out_tiles = out.rearrange("(p i) n -> i p n", i=ROW_TILES)
         for i in range(ROW_TILES):
             logit = add_layer_norm(nc, pools, acc_x[i], gamma_x, hidden_part[i], neg_half, "inp%d" % i)
             gate = pools["work"].tile([P, H], F32, name="gate%d" % i)
             nc.scalar.activation(out=gate[:], in_=logit[:], func=ACT.Sigmoid)
             step = pools["work"].tile([P, H], F32, name="step%d" % i)
-            nc.vector.tensor_mul(out=step[:], in0=gate[:], in1=diff[:, i * H : (i + 1) * H])
+            nc.vector.tensor_mul(out=step[:], in0=gate[:], in1=diff[:, i, :])
             result = pools["work"].tile([P, H], F32, name="result%d" % i)
-            nc.vector.tensor_add(out=result[:], in0=step[:], in1=h_unit[:, i * H : (i + 1) * H])
-            nc.sync.dma_start(out=out[i * P : (i + 1) * P, :], in_=result[:])
+            nc.vector.tensor_add(out=result[:], in0=step[:], in1=h_rows[:, i, :])
+            nc.sync.dma_start(out=out_tiles[i], in_=result[:])

@@ -25,15 +25,16 @@ EPS = 1e-5
 FLOPS = 2 * B * H * (H + IN)
 
 
-def flip(nc, pools, ident, blocks, name):
+def flip(nc, pools, ident, blocks, copy, name):
+    n_blocks = len(blocks)
     flipped = pools["flipped"].tile([P, 2 * BLOCKS, P], F32, tag="flipped")
-    for b in range(BLOCKS):
+    for b in range(n_blocks):
         for u in range(2):
             nc.tensor.transpose(flipped[:, 2 * b + u, :], blocks[b][:, u * P : (u + 1) * P], ident[:])
-    grouped = pools["stage"].tile([P, BLOCKS * P * PACK], BF16, align_bytes=64, name=name + "_grouped")
-    nc.scalar.copy(
-        out=grouped[:].bitcast(F32).rearrange("p (b r u) -> p b r u", b=BLOCKS, u=2),
-        in_=flipped[:].rearrange("p (b u) r -> p b r u", u=2),
+    grouped = pools["stage"].tile([P, n_blocks * P * PACK], BF16, align_bytes=64, name=name + "_grouped")
+    copy(
+        out=grouped[:].bitcast(F32).rearrange("p (b r u) -> p b r u", b=n_blocks, u=2),
+        in_=flipped[:, 0 : 2 * n_blocks, :].rearrange("p (b u) r -> p b r u", u=2),
     )
     return grouped
 
@@ -44,8 +45,8 @@ def mx_tile(pools, width, name):
     return codes, scales
 
 
-def quantise(nc, grouped, mx, first):
-    cols = slice(first, first + BLOCKS * P)
+def quantise(nc, grouped, mx, first, width=BLOCKS * P):
+    cols = slice(first, first + width)
     nc.vector.quantize_mx(out=mx[0][:, cols].bitcast(FP8X4), scales=mx[1][:, cols], in_=grouped[:])
 
 
@@ -60,28 +61,6 @@ def mx_pass(nc, acc, acts, block, weights, start, stop):
         start=start,
         stop=stop,
     )
-
-
-def add_layer_norm(nc, pools, acc, gamma, addend, neg_half, name):
-    stats = pools["small"].tile([P, 6], F32, name=name + "_stats")
-    nc.vector.bn_stats(out=stats[:], in_=acc[:])
-    mean_var = pools["small"].tile([P, 2], F32, name=name + "_mean_var")
-    nc.vector.bn_aggr(out=mean_var[:], in_=stats[:])
-    var_eps = pools["small"].tile([P, 1], F32, name=name + "_var_eps")
-    nc.vector.tensor_scalar_add(var_eps[:], mean_var[:, 1:2], EPS)
-    rstd = pools["small"].tile([P, 1], F32, name=name + "_rstd")
-    nc.gpsimd.tensor_tensor(out=rstd[:], in0=var_eps[:], in1=neg_half[:], op=ALU.pow)
-    centred = pools["work"].tile([P, H], F32, name=name + "_centred")
-    nc.vector.scalar_tensor_tensor(
-        out=centred[:], in0=acc[:], scalar=mean_var[:, 0:1], in1=gamma[:],
-        op0=ALU.subtract, op1=ALU.mult,
-    )
-    total = pools["work"].tile([P, H], F32, name=name + "_total")
-    nc.vector.scalar_tensor_tensor(
-        out=total[:], in0=centred[:], scalar=rstd[:], in1=addend[:],
-        op0=ALU.mult, op1=ALU.add,
-    )
-    return total
 
 
 def spread_vector(nc, pools, ident, vec_cols, v, name):
@@ -107,23 +86,23 @@ def tile_layernormgrucell_pb_s_kernel(tc, x, h, c, W_u, U_u, ln_gamma, ln_beta, 
             "flipped": ctx.enter_context(tc.psum_pool(name="flipped", bufs=4)),
             "acc": ctx.enter_context(tc.psum_pool(name="acc", bufs=1)),
         }
-        const = pools["const"]
-
-        vec_rows = const.tile([P, 2, P], BF16)
-        nc.vector.memset(vec_rows[:], 0.0)
-        nc.sync.dma_start(out=vec_rows[0:8, 0, :], in_=ln_gamma.rearrange("l (q n) -> (l q) n", n=P))
-        nc.sync.dma_start(out=vec_rows[8:12, :, :], in_=ln_beta.rearrange("l (q n) -> q l n", n=P))
+        const, rows, small, work = pools["const"], pools["rows"], pools["small"], pools["work"]
+        ctx.enter_context(tc.manual_schedule())
+        on_scalar, on_vector = nc.scalar.copy, nc.vector.tensor_copy
 
         ident = const.tile([P, P], F32)
         make_identity(nc, ident[:])
-        neg_half = const.tile([P, 1], F32)
+        vec_rows = const.tile([P, 2, P], BF16)
+        nc.vector.memset(vec_rows[:], 0.0)
+        neg_half = const.tile([P, ROW_TILES], F32)
         nc.vector.memset(neg_half[:], -0.5)
         warm = const.tile([P, 1], F32)
-        nc.scalar.activation(out=warm[:], in_=neg_half[:], func=ACT.Sigmoid)
+        nc.scalar.activation(out=warm[:], in_=neg_half[:, 0:1], func=ACT.Sigmoid)
 
-        rows = pools["rows"]
         h_rows = rows.tile([P, ROW_TILES, H], BF16)
         nc.sync.dma_start(out=h_rows[:], in_=h.rearrange("(p i) k -> p i k", i=ROW_TILES))
+        nc.sync.dma_start(out=vec_rows[0:8, 0, :], in_=ln_gamma.rearrange("l (q n) -> (l q) n", n=P))
+        nc.sync.dma_start(out=vec_rows[8:12, :, :], in_=ln_beta.rearrange("l (q n) -> q l n", n=P))
         c_rows = rows.tile([P, ROW_TILES, H], BF16)
         nc.sync.dma_start(out=c_rows[:], in_=c.rearrange("(p i) k -> p i k", i=ROW_TILES))
         w_rows = []
@@ -150,13 +129,14 @@ def tile_layernormgrucell_pb_s_kernel(tc, x, h, c, W_u, U_u, ln_gamma, ln_beta, 
             x_rows.append(xt)
 
         h_mx = mx_tile(pools, ROW_TILES * P, "h")
-        h_grouped = flip(nc, pools, ident, [h_rows[:, i, :].bitcast(F32) for i in range(ROW_TILES)], "h")
-        quantise(nc, h_grouped, h_mx, 0)
-        diff = pools["work"].tile([P, ROW_TILES, H], F32)
-        nc.vector.tensor_sub(out=diff[:], in0=c_rows[:], in1=h_rows[:])
-
+        h_words = [h_rows[:, i, :].bitcast(F32) for i in range(ROW_TILES)]
+        h_grouped = flip(nc, pools, ident, h_words, on_scalar, "h")
         vec_f32 = const.tile([P, P], F32)
         nc.vector.tensor_add(out=vec_f32[:], in0=vec_rows[:, 0, :], in1=vec_rows[:, 1, :])
+        quantise(nc, h_grouped, h_mx, 0)
+        diff = work.tile([P, ROW_TILES, H], F32)
+        nc.gpsimd.tensor_sub(out=diff[:], in0=c_rows[:], in1=h_rows[:])
+
         vec_flipped = pools["flipped"].tile([P, OUT_TILES, P], F32, tag="flipped")
         nc.tensor.transpose(vec_flipped[:, 0, :], vec_f32[:], ident[:])
         vec_cols = const.tile([P, 3 * OUT_TILES], F32)
@@ -164,46 +144,108 @@ def tile_layernormgrucell_pb_s_kernel(tc, x, h, c, W_u, U_u, ln_gamma, ln_beta, 
 
         w_mx = mx_tile(pools, H, "w")
         for n in range(W_UNITS):
-            grouped = flip(nc, pools, ident, [w_rows[n][:, b, :].bitcast(F32) for b in range(BLOCKS)], "w%d" % n)
+            words = [w_rows[n][:, b, :].bitcast(F32) for b in range(BLOCKS)]
+            grouped = flip(nc, pools, ident, words, on_scalar, "w%d" % n)
             quantise(nc, grouped, w_mx, n * BLOCKS * P)
-        gamma_h = spread_vector(nc, pools, ident, vec_cols, 0, "gamma_h")
-        beta_sum = spread_vector(nc, pools, ident, vec_cols, 2, "beta_sum")
-        acc_h = [pools["acc"].tile([P, H], F32, name="acc_h%d" % i) for i in range(ROW_TILES)]
-        for i in range(ROW_TILES):
-            mx_pass(nc, acc_h[i], h_mx, i, w_mx, True, True)
-
-        u_mx = [mx_tile(pools, H, "u%d" % g) for g in range(X_PASSES)]
-        for n in range(W_UNITS):
-            u_words = [u_rows[n][:, b, :].bitcast(F32) for b in range(BLOCKS)]
-            for g in range(X_PASSES):
-                blocks = [words[:, g * 2 * P : (g + 1) * 2 * P] for words in u_words]
-                grouped = flip(nc, pools, ident, blocks, "u%d%d" % (n, g))
-                quantise(nc, grouped, u_mx[g], n * BLOCKS * P)
         gamma_x = spread_vector(nc, pools, ident, vec_cols, 1, "gamma_x")
 
-        hidden_part = [
-            add_layer_norm(nc, pools, acc_h[i], gamma_h, beta_sum, neg_half, "hid%d" % i) for i in range(ROW_TILES)
-        ]
+        u_mx = [mx_tile(pools, H, "u%d" % g) for g in range(X_PASSES)]
 
-        acc_x = []
+        def flip_u(n):
+            u_words = [u_rows[n][:, b, :].bitcast(F32) for b in range(BLOCKS)]
+            return [
+                flip(
+                    nc, pools, ident, [words[:, g * 2 * P : (g + 1) * 2 * P] for words in u_words],
+                    on_vector if (n, g) == (0, 1) else on_scalar, "u%d%d" % (n, g),
+                )
+                for g in range(X_PASSES)
+            ]
+
+        grouped = flip_u(0)
+        acc_h = [pools["acc"].tile([P, H], F32, tag="acc_h%d" % i, name="acc_h%d" % i) for i in range(ROW_TILES)]
+        for i in range(ROW_TILES):
+            mx_pass(nc, acc_h[i], h_mx, i, w_mx, True, True)
+        h_stats = [small.tile([P, 6], F32, name="hid%d_stats" % i) for i in range(ROW_TILES)]
+        mean_var = small.tile([P, ROW_TILES, 2], F32, name="hid_mean_var")
+        var_eps = small.tile([P, ROW_TILES], F32, name="hid_var_eps")
+        rstd = small.tile([P, ROW_TILES], F32, name="hid_rstd")
+        neg_mean = small.tile([P, ROW_TILES], F32, name="hid_neg_mean")
+        shift = small.tile([P, ROW_TILES], F32, name="hid_shift")
+        quantise(nc, grouped[0], u_mx[0], 0)
+        nc.vector.bn_stats(out=h_stats[0][:], in_=acc_h[0][:])
+        nc.vector.bn_stats(out=h_stats[1][:], in_=acc_h[1][:])
+        nc.vector.bn_aggr(out=mean_var[:, 0, :], in_=h_stats[0][:])
+        nc.vector.bn_aggr(out=mean_var[:, 1, :], in_=h_stats[1][:])
+        quantise(nc, grouped[1], u_mx[1], 0)
+        nc.vector.tensor_scalar_add(var_eps[:], mean_var[:, :, 1], EPS)
+        nc.vector.tensor_scalar_mul(neg_mean[:], mean_var[:, :, 0], -1.0)
+        nc.gpsimd.tensor_tensor(out=rstd[:], in0=var_eps[:], in1=neg_half[:], op=ALU.pow)
+        nc.gpsimd.tensor_tensor(out=shift[:], in0=neg_mean[:], in1=rstd[:], op=ALU.mult)
+        grouped = flip_u(1)
+        for g in range(X_PASSES):
+            quantise(nc, grouped[g], u_mx[g], BLOCKS * P)
+
+        x_mx = [mx_tile(pools, X_PASSES * P, "x%d" % i) for i in range(ROW_TILES)]
         for i in range(ROW_TILES):
             x_words = x_rows[i][:].bitcast(F32)
             blocks = [x_words[:, g * 2 * P : (g + 1) * 2 * P] for g in range(X_PASSES)]
-            grouped = flip(nc, pools, ident, blocks, "x%d" % i)
-            x_mx = mx_tile(pools, X_PASSES * P, "x%d" % i)
-            quantise(nc, grouped, x_mx, 0)
-            acc = pools["acc"].tile([P, H], F32, name="acc_x%d" % i)
-            for g in range(X_PASSES):
-                mx_pass(nc, acc, x_mx, g, u_mx[g], g == 0, g == X_PASSES - 1)
-            acc_x.append(acc)
+            quantise(nc, flip(nc, pools, ident, blocks, on_scalar, "x%d" % i), x_mx[i], 0)
 
+        acc_x, turned_ps, hidden_part = [], [], []
+        for i in range(ROW_TILES):
+            acc_x.append(pools["acc"].tile([P, H], F32, name="acc_x%d" % i))
+            for g in range(X_PASSES):
+                mx_pass(nc, acc_x[i], x_mx[i], g, u_mx[g], g == 0, g == X_PASSES - 1)
+        for i in range(ROW_TILES):
+            normed = work.tile([P, OUT_TILES, P], F32, name="hid%d_normed" % i)
+            nc.scalar.activation(
+                out=normed[:].rearrange("p q n -> p (q n)"), in_=acc_h[i][:], func=ACT.Identity,
+                scale=rstd[:, i : i + 1], bias=shift[:, i : i + 1],
+            )
+            turned_ps.append(pools["flipped"].tile([P, OUT_TILES, P], F32, tag="flipped", name="turned_ps%d" % i))
+            for q in range(OUT_TILES):
+                nc.tensor.transpose(turned_ps[i][:, q, :], normed[:, q, :], ident[:])
+        for i in range(ROW_TILES):
+            turned = work.tile([P, OUT_TILES, P], F32, name="hid%d_turned" % i)
+            for q in range(OUT_TILES):
+                nc.scalar.activation(
+                    out=turned[:, q, :], in_=turned_ps[i][:, q, :], func=ACT.Identity,
+                    scale=vec_cols[:, q : q + 1], bias=vec_cols[:, 2 * OUT_TILES + q : 2 * OUT_TILES + q + 1],
+                )
+            hidden = pools["acc"].tile([P, OUT_TILES, P], F32, tag="acc_h%d" % i, name="hidden%d" % i)
+            for q in range(OUT_TILES):
+                nc.tensor.transpose(hidden[:, q, :], turned[:, q, :], ident[:])
+            hidden_part.append(hidden[:].rearrange("p q n -> p (q n)"))
+
+        x_stats = [small.tile([P, 6], F32, name="inp%d_stats" % i) for i in range(ROW_TILES)]
+        x_mean_var = small.tile([P, ROW_TILES, 2], F32, name="inp_mean_var")
+        x_var_eps = small.tile([P, ROW_TILES], F32, name="inp_var_eps")
+        x_rstd = small.tile([P, ROW_TILES], F32, name="inp_rstd")
+        centred = [work.tile([P, H], F32, name="centred%d" % i) for i in range(ROW_TILES)]
+        logit = [work.tile([P, H], F32, name="logit%d" % i) for i in range(ROW_TILES)]
+        gate = [work.tile([P, H], F32, name="gate%d" % i) for i in range(ROW_TILES)]
+        step = [work.tile([P, H], F32, name="step%d" % i) for i in range(ROW_TILES)]
+        result = [work.tile([P, H], F32, name="result%d" % i) for i in range(ROW_TILES)]
         out_tiles = out.rearrange("(p i) n -> i p n", i=ROW_TILES)
         for i in range(ROW_TILES):
-            logit = add_layer_norm(nc, pools, acc_x[i], gamma_x, hidden_part[i], neg_half, "inp%d" % i)
-            gate = pools["work"].tile([P, H], F32, name="gate%d" % i)
-            nc.scalar.activation(out=gate[:], in_=logit[:], func=ACT.Sigmoid)
-            step = pools["work"].tile([P, H], F32, name="step%d" % i)
-            nc.vector.tensor_mul(out=step[:], in0=gate[:], in1=diff[:, i, :])
-            result = pools["work"].tile([P, H], F32, name="result%d" % i)
-            nc.vector.tensor_add(out=result[:], in0=step[:], in1=h_rows[:, i, :])
-            nc.sync.dma_start(out=out_tiles[i], in_=result[:])
+            nc.vector.bn_stats(out=x_stats[i][:], in_=acc_x[i][:])
+        for i in range(ROW_TILES):
+            nc.vector.bn_aggr(out=x_mean_var[:, i, :], in_=x_stats[i][:])
+        nc.vector.tensor_scalar_add(x_var_eps[:], x_mean_var[:, :, 1], EPS)
+        nc.gpsimd.tensor_tensor(out=x_rstd[:], in0=x_var_eps[:], in1=neg_half[:], op=ALU.pow)
+        for i in range(ROW_TILES):
+            nc.vector.scalar_tensor_tensor(
+                out=centred[i][:], in0=acc_x[i][:], scalar=x_mean_var[:, i, 0:1], in1=gamma_x[:],
+                op0=ALU.subtract, op1=ALU.mult,
+            )
+        for i in range(ROW_TILES):
+            nc.vector.scalar_tensor_tensor(
+                out=logit[i][:], in0=centred[i][:], scalar=x_rstd[:, i : i + 1], in1=hidden_part[i],
+                op0=ALU.mult, op1=ALU.add,
+            )
+            nc.scalar.activation(out=gate[i][:], in_=logit[i][:], func=ACT.Sigmoid)
+        for i in range(ROW_TILES):
+            nc.vector.tensor_mul(out=step[i][:], in0=gate[i][:], in1=diff[:, i, :])
+        for i in range(ROW_TILES):
+            nc.vector.tensor_add(out=result[i][:], in0=step[i][:], in1=h_rows[:, i, :])
+            nc.sync.dma_start(out=out_tiles[i], in_=result[i][:])

@@ -133,9 +133,9 @@ def tile_layernormgrucell_pb_s_kernel(tc, x, h, c, W_u, U_u, ln_gamma, ln_beta, 
         h_grouped = flip(nc, pools, ident, h_words, on_scalar, "h")
         vec_f32 = const.tile([P, P], F32)
         nc.vector.tensor_add(out=vec_f32[:], in0=vec_rows[:, 0, :], in1=vec_rows[:, 1, :])
-        quantise(nc, h_grouped, h_mx, 0)
         diff = work.tile([P, ROW_TILES, H], F32)
-        nc.gpsimd.tensor_sub(out=diff[:], in0=c_rows[:], in1=h_rows[:])
+        nc.vector.tensor_sub(out=diff[:], in0=c_rows[:], in1=h_rows[:])
+        quantise(nc, h_grouped, h_mx, 0)
 
         vec_flipped = pools["flipped"].tile([P, OUT_TILES, P], F32, tag="flipped")
         nc.tensor.transpose(vec_flipped[:, 0, :], vec_f32[:], ident[:])

@@ -45,9 +45,9 @@ def mx_tile(pools, width, name):
     return codes, scales
 
 
-def quantise(nc, grouped, mx, first, width=BLOCKS * P):
-    cols = slice(first, first + width)
-    nc.vector.quantize_mx(out=mx[0][:, cols].bitcast(FP8X4), scales=mx[1][:, cols], in_=grouped[:])
+def quantise(nc, grouped, mx, first):
+    cols = slice(first, first + grouped.shape[-1] // PACK)
+    nc.vector.quantize_mx(out=mx[0][:, cols].bitcast(FP8X4), scales=mx[1][:, cols], in_=grouped)
 
 
 def mx_pass(nc, acc, acts, block, weights, start, stop):
@@ -96,6 +96,15 @@ def tile_layernormgrucell_pb_s_kernel(tc, x, h, c, W_u, U_u, ln_gamma, ln_beta, 
         nc.vector.memset(vec_rows[:], 0.0)
         neg_half = const.tile([P, ROW_TILES], F32)
         nc.vector.memset(neg_half[:], -0.5)
+        zeros = const.tile([P, P], F32)
+        nc.vector.memset(zeros[:], 0.0)
+        idle_ps = pools["acc"].tile([P, P], F32, tag="acc_x0", name="idle_ps")
+
+        def keep_busy(count):
+            for rep in range(count):
+                nc.tensor.matmul(out=idle_ps[:], lhsT=zeros[:], rhs=zeros[:], start=True, stop=True)
+
+        keep_busy(3)
         warm = const.tile([P, 1], F32)
         nc.scalar.activation(out=warm[:], in_=neg_half[:, 0:1], func=ACT.Sigmoid)
 
@@ -114,12 +123,9 @@ def tile_layernormgrucell_pb_s_kernel(tc, x, h, c, W_u, U_u, ln_gamma, ln_beta, 
             )
             w_rows.append(w)
         u_rows = []
-        for n in range(W_UNITS):
-            u = rows.tile([P, BLOCKS, IN], BF16, name="u%d" % n)
-            nc.sync.dma_start(
-                out=u[:],
-                in_=U_u[n * BLOCKS * P : (n + 1) * BLOCKS * P, :].rearrange("(b p) k -> p b k", p=P),
-            )
+        for n in range(OUT_TILES):
+            u = rows.tile([P, IN], BF16, name="u%d" % n)
+            nc.sync.dma_start(out=u[:], in_=U_u[n * P : (n + 1) * P, :])
             u_rows.append(u)
         x_rows = []
         x_tiles = x.rearrange("(p i) k -> i p k", i=ROW_TILES)
@@ -135,33 +141,32 @@ def tile_layernormgrucell_pb_s_kernel(tc, x, h, c, W_u, U_u, ln_gamma, ln_beta, 
         nc.vector.tensor_add(out=vec_f32[:], in0=vec_rows[:, 0, :], in1=vec_rows[:, 1, :])
         diff = work.tile([P, ROW_TILES, H], F32)
         nc.vector.tensor_sub(out=diff[:], in0=c_rows[:], in1=h_rows[:])
-        quantise(nc, h_grouped, h_mx, 0)
+        quantise(nc, h_grouped[:], h_mx, 0)
 
         vec_flipped = pools["flipped"].tile([P, OUT_TILES, P], F32, tag="flipped")
         nc.tensor.transpose(vec_flipped[:, 0, :], vec_f32[:], ident[:])
         vec_cols = const.tile([P, 3 * OUT_TILES], F32)
         nc.scalar.copy(out=vec_cols[:], in_=vec_flipped[:, 0, 0 : 3 * OUT_TILES])
 
+        keep_busy(2)
         w_mx = mx_tile(pools, H, "w")
         for n in range(W_UNITS):
             words = [w_rows[n][:, b, :].bitcast(F32) for b in range(BLOCKS)]
             grouped = flip(nc, pools, ident, words, on_scalar, "w%d" % n)
-            quantise(nc, grouped, w_mx, n * BLOCKS * P)
-        gamma_x = spread_vector(nc, pools, ident, vec_cols, 1, "gamma_x")
+            quantise(nc, grouped[:], w_mx, n * BLOCKS * P)
 
         u_mx = [mx_tile(pools, H, "u%d" % g) for g in range(X_PASSES)]
 
-        def flip_u(n):
-            u_words = [u_rows[n][:, b, :].bitcast(F32) for b in range(BLOCKS)]
-            return [
-                flip(
-                    nc, pools, ident, [words[:, g * 2 * P : (g + 1) * 2 * P] for words in u_words],
-                    on_vector if (n, g) == (0, 1) else on_scalar, "u%d%d" % (n, g),
-                )
-                for g in range(X_PASSES)
-            ]
+        def flip_in(row_tile, copy, name):
+            words = row_tile[:].bitcast(F32)
+            return flip(nc, pools, ident, [words[:, g * 2 * P : (g + 1) * 2 * P] for g in range(X_PASSES)], copy, name)
 
-        grouped = flip_u(0)
+        def quantise_u(n):
+            for g in range(X_PASSES):
+                quantise(nc, u_grouped[n][:, g * K_PASS : (g + 1) * K_PASS], u_mx[g], n * P)
+
+        keep_busy(2)
+        u_grouped = [flip_in(u_rows[n], on_scalar, "u%d" % n) for n in range(OUT_TILES - 1)]
         acc_h = [pools["acc"].tile([P, H], F32, tag="acc_h%d" % i, name="acc_h%d" % i) for i in range(ROW_TILES)]
         for i in range(ROW_TILES):
             mx_pass(nc, acc_h[i], h_mx, i, w_mx, True, True)
@@ -171,29 +176,29 @@ def tile_layernormgrucell_pb_s_kernel(tc, x, h, c, W_u, U_u, ln_gamma, ln_beta, 
         rstd = small.tile([P, ROW_TILES], F32, name="hid_rstd")
         neg_mean = small.tile([P, ROW_TILES], F32, name="hid_neg_mean")
         shift = small.tile([P, ROW_TILES], F32, name="hid_shift")
-        quantise(nc, grouped[0], u_mx[0], 0)
+        quantise_u(0)
         nc.vector.bn_stats(out=h_stats[0][:], in_=acc_h[0][:])
         nc.vector.bn_stats(out=h_stats[1][:], in_=acc_h[1][:])
         nc.vector.bn_aggr(out=mean_var[:, 0, :], in_=h_stats[0][:])
         nc.vector.bn_aggr(out=mean_var[:, 1, :], in_=h_stats[1][:])
-        quantise(nc, grouped[1], u_mx[1], 0)
+        quantise_u(1)
         nc.vector.tensor_scalar_add(var_eps[:], mean_var[:, :, 1], EPS)
         nc.vector.tensor_scalar_mul(neg_mean[:], mean_var[:, :, 0], -1.0)
         nc.gpsimd.tensor_tensor(out=rstd[:], in0=var_eps[:], in1=neg_half[:], op=ALU.pow)
         nc.gpsimd.tensor_tensor(out=shift[:], in0=neg_mean[:], in1=rstd[:], op=ALU.mult)
-        grouped = flip_u(1)
-        for g in range(X_PASSES):
-            quantise(nc, grouped[g], u_mx[g], BLOCKS * P)
+        quantise_u(2)
+        u_grouped.append(flip_in(u_rows[3], on_scalar, "u3"))
+        quantise_u(3)
 
         x_mx = [mx_tile(pools, X_PASSES * P, "x%d" % i) for i in range(ROW_TILES)]
         for i in range(ROW_TILES):
-            x_words = x_rows[i][:].bitcast(F32)
-            blocks = [x_words[:, g * 2 * P : (g + 1) * 2 * P] for g in range(X_PASSES)]
-            quantise(nc, flip(nc, pools, ident, blocks, on_scalar, "x%d" % i), x_mx[i], 0)
+            quantise(nc, flip_in(x_rows[i], on_scalar, "x%d" % i)[:], x_mx[i], 0)
+
+        gamma_x = spread_vector(nc, pools, ident, vec_cols, 1, "gamma_x")
 
         acc_x, turned_ps, hidden_part = [], [], []
         for i in range(ROW_TILES):
-            acc_x.append(pools["acc"].tile([P, H], F32, name="acc_x%d" % i))
+            acc_x.append(pools["acc"].tile([P, H], F32, tag="acc_x%d" % i, name="acc_x%d" % i))
             for g in range(X_PASSES):
                 mx_pass(nc, acc_x[i], x_mx[i], g, u_mx[g], g == 0, g == X_PASSES - 1)
         for i in range(ROW_TILES):

@@ -90,14 +90,14 @@ def tile_layernormgrucell_pb_s_kernel(tc, x, h, c, W_u, U_u, ln_gamma, ln_beta, 
         ctx.enter_context(tc.manual_schedule())
         on_scalar, on_vector = nc.scalar.copy, nc.vector.tensor_copy
 
+        zeros = const.tile([P, P], F32)
+        nc.vector.memset(zeros[:], 0.0)
         ident = const.tile([P, P], F32)
         make_identity(nc, ident[:])
         vec_rows = const.tile([P, 2, P], BF16)
         nc.vector.memset(vec_rows[:], 0.0)
         neg_half = const.tile([P, ROW_TILES], F32)
         nc.vector.memset(neg_half[:], -0.5)
-        zeros = const.tile([P, P], F32)
-        nc.vector.memset(zeros[:], 0.0)
         idle_ps = pools["acc"].tile([P, P], F32, tag="acc_x0", name="idle_ps")
 
         def keep_busy(count):
@@ -105,6 +105,9 @@ def tile_layernormgrucell_pb_s_kernel(tc, x, h, c, W_u, U_u, ln_gamma, ln_beta, 
                 nc.tensor.matmul(out=idle_ps[:], lhsT=zeros[:], rhs=zeros[:], start=True, stop=True)
 
         keep_busy(3)
+        stats = const.tile([P, 2 * ROW_TILES, 9], F32)
+        nc.vector.memset(stats[:], 0.0)
+        nc.vector.memset(stats[:, :, 8:9], H * EPS)
         warm = const.tile([P, 1], F32)
         nc.scalar.activation(out=warm[:], in_=neg_half[:, 0:1], func=ACT.Sigmoid)
 
@@ -112,8 +115,6 @@ def tile_layernormgrucell_pb_s_kernel(tc, x, h, c, W_u, U_u, ln_gamma, ln_beta, 
         nc.sync.dma_start(out=h_rows[:], in_=h.rearrange("(p i) k -> p i k", i=ROW_TILES))
         nc.sync.dma_start(out=vec_rows[0:8, 0, :], in_=ln_gamma.rearrange("l (q n) -> (l q) n", n=P))
         nc.sync.dma_start(out=vec_rows[8:12, :, :], in_=ln_beta.rearrange("l (q n) -> q l n", n=P))
-        c_rows = rows.tile([P, ROW_TILES, H], BF16)
-        nc.sync.dma_start(out=c_rows[:], in_=c.rearrange("(p i) k -> p i k", i=ROW_TILES))
         w_rows = []
         for n in range(W_UNITS):
             w = rows.tile([P, BLOCKS, H], BF16, name="w%d" % n)
@@ -133,27 +134,27 @@ def tile_layernormgrucell_pb_s_kernel(tc, x, h, c, W_u, U_u, ln_gamma, ln_beta, 
             xt = rows.tile([P, IN], BF16, name="x%d" % i)
             nc.sync.dma_start(out=xt[:], in_=x_tiles[i])
             x_rows.append(xt)
+        c_rows = rows.tile([P, ROW_TILES, H], BF16)
+        nc.sync.dma_start(out=c_rows[:], in_=c.rearrange("(p i) k -> p i k", i=ROW_TILES))
 
         h_mx = mx_tile(pools, ROW_TILES * P, "h")
         h_words = [h_rows[:, i, :].bitcast(F32) for i in range(ROW_TILES)]
         h_grouped = flip(nc, pools, ident, h_words, on_scalar, "h")
         vec_f32 = const.tile([P, P], F32)
         nc.vector.tensor_add(out=vec_f32[:], in0=vec_rows[:, 0, :], in1=vec_rows[:, 1, :])
-        diff = work.tile([P, ROW_TILES, H], F32)
-        nc.vector.tensor_sub(out=diff[:], in0=c_rows[:], in1=h_rows[:])
         quantise(nc, h_grouped[:], h_mx, 0)
 
-        vec_flipped = pools["flipped"].tile([P, OUT_TILES, P], F32, tag="flipped")
-        nc.tensor.transpose(vec_flipped[:, 0, :], vec_f32[:], ident[:])
-        vec_cols = const.tile([P, 3 * OUT_TILES], F32)
-        nc.scalar.copy(out=vec_cols[:], in_=vec_flipped[:, 0, 0 : 3 * OUT_TILES])
-
-        keep_busy(2)
         w_mx = mx_tile(pools, H, "w")
         for n in range(W_UNITS):
             words = [w_rows[n][:, b, :].bitcast(F32) for b in range(BLOCKS)]
             grouped = flip(nc, pools, ident, words, on_scalar, "w%d" % n)
             quantise(nc, grouped[:], w_mx, n * BLOCKS * P)
+            keep_busy(1)
+
+        vec_flipped = pools["flipped"].tile([P, OUT_TILES, P], F32, tag="flipped")
+        nc.tensor.transpose(vec_flipped[:, 0, :], vec_f32[:], ident[:])
+        vec_cols = const.tile([P, 3 * OUT_TILES], F32)
+        nc.scalar.copy(out=vec_cols[:], in_=vec_flipped[:, 0, 0 : 3 * OUT_TILES])
 
         u_mx = [mx_tile(pools, H, "u%d" % g) for g in range(X_PASSES)]
 
@@ -165,26 +166,22 @@ def tile_layernormgrucell_pb_s_kernel(tc, x, h, c, W_u, U_u, ln_gamma, ln_beta, 
             for g in range(X_PASSES):
                 quantise(nc, u_grouped[n][:, g * K_PASS : (g + 1) * K_PASS], u_mx[g], n * P)
 
-        keep_busy(2)
         u_grouped = [flip_in(u_rows[n], on_scalar, "u%d" % n) for n in range(OUT_TILES - 1)]
         acc_h = [pools["acc"].tile([P, H], F32, tag="acc_h%d" % i, name="acc_h%d" % i) for i in range(ROW_TILES)]
         for i in range(ROW_TILES):
             mx_pass(nc, acc_h[i], h_mx, i, w_mx, True, True)
-        h_stats = [small.tile([P, 6], F32, name="hid%d_stats" % i) for i in range(ROW_TILES)]
         mean_var = small.tile([P, ROW_TILES, 2], F32, name="hid_mean_var")
-        var_eps = small.tile([P, ROW_TILES], F32, name="hid_var_eps")
         rstd = small.tile([P, ROW_TILES], F32, name="hid_rstd")
         neg_mean = small.tile([P, ROW_TILES], F32, name="hid_neg_mean")
         shift = small.tile([P, ROW_TILES], F32, name="hid_shift")
         quantise_u(0)
-        nc.vector.bn_stats(out=h_stats[0][:], in_=acc_h[0][:])
-        nc.vector.bn_stats(out=h_stats[1][:], in_=acc_h[1][:])
-        nc.vector.bn_aggr(out=mean_var[:, 0, :], in_=h_stats[0][:])
-        nc.vector.bn_aggr(out=mean_var[:, 1, :], in_=h_stats[1][:])
+        nc.vector.bn_stats(out=stats[:, 0, 0:6], in_=acc_h[0][:])
+        nc.vector.bn_stats(out=stats[:, 1, 0:6], in_=acc_h[1][:])
+        nc.vector.bn_aggr(out=mean_var[:, 0, :], in_=stats[:, 0, :])
+        nc.vector.bn_aggr(out=mean_var[:, 1, :], in_=stats[:, 1, :])
         quantise_u(1)
-        nc.vector.tensor_scalar_add(var_eps[:], mean_var[:, :, 1], EPS)
         nc.vector.tensor_scalar_mul(neg_mean[:], mean_var[:, :, 0], -1.0)
-        nc.gpsimd.tensor_tensor(out=rstd[:], in0=var_eps[:], in1=neg_half[:], op=ALU.pow)
+        nc.gpsimd.tensor_tensor(out=rstd[:], in0=mean_var[:, :, 1], in1=neg_half[:], op=ALU.pow)
         nc.gpsimd.tensor_tensor(out=shift[:], in0=neg_mean[:], in1=rstd[:], op=ALU.mult)
         quantise_u(2)
         u_grouped.append(flip_in(u_rows[3], on_scalar, "u3"))
@@ -222,9 +219,7 @@ def tile_layernormgrucell_pb_s_kernel(tc, x, h, c, W_u, U_u, ln_gamma, ln_beta, 
                 nc.tensor.transpose(hidden[:, q, :], turned[:, q, :], ident[:])
             hidden_part.append(hidden[:].rearrange("p q n -> p (q n)"))
 
-        x_stats = [small.tile([P, 6], F32, name="inp%d_stats" % i) for i in range(ROW_TILES)]
         x_mean_var = small.tile([P, ROW_TILES, 2], F32, name="inp_mean_var")
-        x_var_eps = small.tile([P, ROW_TILES], F32, name="inp_var_eps")
         x_rstd = small.tile([P, ROW_TILES], F32, name="inp_rstd")
         centred = [work.tile([P, H], F32, name="centred%d" % i) for i in range(ROW_TILES)]
         logit = [work.tile([P, H], F32, name="logit%d" % i) for i in range(ROW_TILES)]
@@ -232,12 +227,14 @@ def tile_layernormgrucell_pb_s_kernel(tc, x, h, c, W_u, U_u, ln_gamma, ln_beta, 
         step = [work.tile([P, H], F32, name="step%d" % i) for i in range(ROW_TILES)]
         result = [work.tile([P, H], F32, name="result%d" % i) for i in range(ROW_TILES)]
         out_tiles = out.rearrange("(p i) n -> i p n", i=ROW_TILES)
+        diff = [work.tile([P, H], F32, name="diff%d" % i) for i in range(ROW_TILES)]
+        nc.gpsimd.tensor_sub(out=diff[0][:], in0=c_rows[:, 0, :], in1=h_rows[:, 0, :])
         for i in range(ROW_TILES):
-            nc.vector.bn_stats(out=x_stats[i][:], in_=acc_x[i][:])
+            nc.vector.bn_stats(out=stats[:, ROW_TILES + i, 0:6], in_=acc_x[i][:])
         for i in range(ROW_TILES):
-            nc.vector.bn_aggr(out=x_mean_var[:, i, :], in_=x_stats[i][:])
-        nc.vector.tensor_scalar_add(x_var_eps[:], x_mean_var[:, :, 1], EPS)
-        nc.gpsimd.tensor_tensor(out=x_rstd[:], in0=x_var_eps[:], in1=neg_half[:], op=ALU.pow)
+            nc.vector.bn_aggr(out=x_mean_var[:, i, :], in_=stats[:, ROW_TILES + i, :])
+        nc.gpsimd.tensor_tensor(out=x_rstd[:], in0=x_mean_var[:, :, 1], in1=neg_half[:], op=ALU.pow)
+        nc.gpsimd.tensor_sub(out=diff[1][:], in0=c_rows[:, 1, :], in1=h_rows[:, 1, :])
         for i in range(ROW_TILES):
             nc.vector.scalar_tensor_tensor(
                 out=centred[i][:], in0=acc_x[i][:], scalar=x_mean_var[:, i, 0:1], in1=gamma_x[:],
@@ -250,7 +247,7 @@ def tile_layernormgrucell_pb_s_kernel(tc, x, h, c, W_u, U_u, ln_gamma, ln_beta, 
             )
             nc.scalar.activation(out=gate[i][:], in_=logit[i][:], func=ACT.Sigmoid)
         for i in range(ROW_TILES):
-            nc.vector.tensor_mul(out=step[i][:], in0=gate[i][:], in1=diff[:, i, :])
+            nc.vector.tensor_mul(out=step[i][:], in0=gate[i][:], in1=diff[i][:])
         for i in range(ROW_TILES):
             nc.vector.tensor_add(out=result[i][:], in0=step[i][:], in1=h_rows[:, i, :])
             nc.sync.dma_start(out=out_tiles[i], in_=result[i][:])

@@ -31,7 +31,7 @@ def flip(nc, pools, ident, blocks, copy, name):
     for b in range(n_blocks):
         for u in range(2):
             nc.tensor.transpose(flipped[:, 2 * b + u, :], blocks[b][:, u * P : (u + 1) * P], ident[:])
-    grouped = pools["stage"].tile([P, n_blocks * P * PACK], BF16, align_bytes=64, name=name + "_grouped")
+    grouped = pools["stage"].tile([P, n_blocks * P * PACK], BF16, align_bytes=64, tag=name + "_grouped", name=name + "_grouped")
     copy(
         out=grouped[:].bitcast(F32).rearrange("p (b r u) -> p b r u", b=n_blocks, u=2),
         in_=flipped[:, 0 : 2 * n_blocks, :].rearrange("p (b u) r -> p b r u", u=2),
@@ -50,14 +50,14 @@ def quantise(nc, grouped, mx, first):
     nc.vector.quantize_mx(out=mx[0][:, cols].bitcast(FP8X4), scales=mx[1][:, cols], in_=grouped)
 
 
-def mx_pass(nc, acc, acts, block, weights, start, stop):
+def mx_pass(nc, acc, acts, block, weights, outs, start, stop):
     cols = slice(block * P, (block + 1) * P)
     nc.tensor.matmul_mx(
-        out=acc[:],
+        out=acc,
         lhsT=acts[0][:, cols].bitcast(FP8X4),
         lhsT_scale=acts[1][:, cols],
-        rhs=weights[0][:].bitcast(FP8X4),
-        rhs_scale=weights[1][:],
+        rhs=weights[0][:, outs].bitcast(FP8X4),
+        rhs_scale=weights[1][:, outs],
         start=start,
         stop=stop,
     )
@@ -112,9 +112,8 @@ def tile_layernormgrucell_pb_s_kernel(tc, x, h, c, W_u, U_u, ln_gamma, ln_beta, 
         nc.scalar.activation(out=warm[:], in_=neg_half[:, 0:1], func=ACT.Sigmoid)
 
         h_rows = rows.tile([P, ROW_TILES, H], BF16)
-        nc.sync.dma_start(out=h_rows[:], in_=h.rearrange("(p i) k -> p i k", i=ROW_TILES))
-        nc.sync.dma_start(out=vec_rows[0:8, 0, :], in_=ln_gamma.rearrange("l (q n) -> (l q) n", n=P))
-        nc.sync.dma_start(out=vec_rows[8:12, :, :], in_=ln_beta.rearrange("l (q n) -> q l n", n=P))
+        for i in range(ROW_TILES):
+            nc.sync.dma_start(out=h_rows[:, i, :], in_=h.rearrange("(p i) k -> i p k", i=ROW_TILES)[i])
         w_rows = []
         for n in range(W_UNITS):
             w = rows.tile([P, BLOCKS, H], BF16, name="w%d" % n)
@@ -123,26 +122,35 @@ def tile_layernormgrucell_pb_s_kernel(tc, x, h, c, W_u, U_u, ln_gamma, ln_beta, 
                 in_=W_u[n * BLOCKS * P : (n + 1) * BLOCKS * P, :].rearrange("(b p) k -> p b k", p=P),
             )
             w_rows.append(w)
+        nc.sync.dma_start(out=vec_rows[0:8, 0, :], in_=ln_gamma.rearrange("l (q n) -> (l q) n", n=P))
+        nc.sync.dma_start(out=vec_rows[8:12, :, :], in_=ln_beta.rearrange("l (q n) -> q l n", n=P))
         u_rows = []
-        for n in range(OUT_TILES):
-            u = rows.tile([P, IN], BF16, name="u%d" % n)
-            nc.sync.dma_start(out=u[:], in_=U_u[n * P : (n + 1) * P, :])
-            u_rows.append(u)
         x_rows = []
         x_tiles = x.rearrange("(p i) k -> i p k", i=ROW_TILES)
+
+        def load_u(n):
+            u_rows.append(rows.tile([P, IN], BF16, name="u%d" % n))
+            nc.sync.dma_start(out=u_rows[n][:], in_=U_u[n * P : (n + 1) * P, :])
+
+        def load_x(i):
+            x_rows.append(rows.tile([P, IN], BF16, name="x%d" % i))
+            nc.sync.dma_start(out=x_rows[i][:], in_=x_tiles[i])
+
+        for n in range(OUT_TILES - 1):
+            load_u(n)
+        load_x(0)
+        load_u(OUT_TILES - 1)
+        load_x(1)
+        c_rows = [rows.tile([P, H], BF16, name="c%d" % i) for i in range(ROW_TILES)]
         for i in range(ROW_TILES):
-            xt = rows.tile([P, IN], BF16, name="x%d" % i)
-            nc.sync.dma_start(out=xt[:], in_=x_tiles[i])
-            x_rows.append(xt)
-        c_rows = rows.tile([P, ROW_TILES, H], BF16)
-        nc.sync.dma_start(out=c_rows[:], in_=c.rearrange("(p i) k -> p i k", i=ROW_TILES))
+            nc.sync.dma_start(out=c_rows[i][:], in_=c.rearrange("(p i) k -> i p k", i=ROW_TILES)[i])
 
         h_mx = mx_tile(pools, ROW_TILES * P, "h")
-        h_words = [h_rows[:, i, :].bitcast(F32) for i in range(ROW_TILES)]
-        h_grouped = flip(nc, pools, ident, h_words, on_scalar, "h")
+        for i in range(ROW_TILES):
+            quantise(nc, flip(nc, pools, ident, [h_rows[:, i, :].bitcast(F32)], on_scalar, "h%d" % i)[:], h_mx, i * P)
+
         vec_f32 = const.tile([P, P], F32)
         nc.vector.tensor_add(out=vec_f32[:], in0=vec_rows[:, 0, :], in1=vec_rows[:, 1, :])
-        quantise(nc, h_grouped[:], h_mx, 0)
 
         w_mx = mx_tile(pools, H, "w")
         for n in range(W_UNITS):
@@ -156,48 +164,54 @@ def tile_layernormgrucell_pb_s_kernel(tc, x, h, c, W_u, U_u, ln_gamma, ln_beta, 
         vec_cols = const.tile([P, 3 * OUT_TILES], F32)
         nc.scalar.copy(out=vec_cols[:], in_=vec_flipped[:, 0, 0 : 3 * OUT_TILES])
 
-        u_mx = [mx_tile(pools, H, "u%d" % g) for g in range(X_PASSES)]
+        u_mx = [mx_tile(pools, X_PASSES * P, "u%d" % n) for n in range(OUT_TILES)]
 
         def flip_in(row_tile, copy, name):
             words = row_tile[:].bitcast(F32)
             return flip(nc, pools, ident, [words[:, g * 2 * P : (g + 1) * 2 * P] for g in range(X_PASSES)], copy, name)
 
         def quantise_u(n):
-            for g in range(X_PASSES):
-                quantise(nc, u_grouped[n][:, g * K_PASS : (g + 1) * K_PASS], u_mx[g], n * P)
+            quantise(nc, u_grouped[n][:], u_mx[n], 0)
 
         u_grouped = [flip_in(u_rows[n], on_scalar, "u%d" % n) for n in range(OUT_TILES - 1)]
         acc_h = [pools["acc"].tile([P, H], F32, tag="acc_h%d" % i, name="acc_h%d" % i) for i in range(ROW_TILES)]
         for i in range(ROW_TILES):
-            mx_pass(nc, acc_h[i], h_mx, i, w_mx, True, True)
+            mx_pass(nc, acc_h[i][:], h_mx, i, w_mx, slice(0, H), True, True)
         mean_var = small.tile([P, ROW_TILES, 2], F32, name="hid_mean_var")
         rstd = small.tile([P, ROW_TILES], F32, name="hid_rstd")
         neg_mean = small.tile([P, ROW_TILES], F32, name="hid_neg_mean")
         shift = small.tile([P, ROW_TILES], F32, name="hid_shift")
         quantise_u(0)
+        quantise_u(1)
         nc.vector.bn_stats(out=stats[:, 0, 0:6], in_=acc_h[0][:])
         nc.vector.bn_stats(out=stats[:, 1, 0:6], in_=acc_h[1][:])
         nc.vector.bn_aggr(out=mean_var[:, 0, :], in_=stats[:, 0, :])
         nc.vector.bn_aggr(out=mean_var[:, 1, :], in_=stats[:, 1, :])
-        quantise_u(1)
         nc.vector.tensor_scalar_mul(neg_mean[:], mean_var[:, :, 0], -1.0)
         nc.gpsimd.tensor_tensor(out=rstd[:], in0=mean_var[:, :, 1], in1=neg_half[:], op=ALU.pow)
         nc.gpsimd.tensor_tensor(out=shift[:], in0=neg_mean[:], in1=rstd[:], op=ALU.mult)
         quantise_u(2)
-        u_grouped.append(flip_in(u_rows[3], on_scalar, "u3"))
-        quantise_u(3)
 
         x_mx = [mx_tile(pools, X_PASSES * P, "x%d" % i) for i in range(ROW_TILES)]
-        for i in range(ROW_TILES):
-            quantise(nc, flip_in(x_rows[i], on_scalar, "x%d" % i)[:], x_mx[i], 0)
+        quantise(nc, flip_in(x_rows[0], on_scalar, "x0")[:], x_mx[0], 0)
+        u_grouped.append(flip_in(u_rows[3], on_scalar, "u3"))
+        quantise_u(3)
+        quantise(nc, flip_in(x_rows[1], on_scalar, "x1")[:], x_mx[1], 0)
+        diff = [pools["stage"].tile([P, H], F32, tag="x1_grouped", align_bytes=64, name="diff0")]
+        nc.gpsimd.tensor_sub(out=diff[0][:], in0=c_rows[0][:], in1=h_rows[:, 0, :])
 
         gamma_x = spread_vector(nc, pools, ident, vec_cols, 1, "gamma_x")
+        keep_busy(2)
 
         acc_x, turned_ps, hidden_part = [], [], []
         for i in range(ROW_TILES):
             acc_x.append(pools["acc"].tile([P, H], F32, tag="acc_x%d" % i, name="acc_x%d" % i))
-            for g in range(X_PASSES):
-                mx_pass(nc, acc_x[i], x_mx[i], g, u_mx[g], g == 0, g == X_PASSES - 1)
+            for n in range(OUT_TILES):
+                for g in range(X_PASSES):
+                    mx_pass(
+                        nc, acc_x[i][:, n * P : (n + 1) * P], x_mx[i], g, u_mx[n], slice(g * P, (g + 1) * P),
+                        g == 0, g == X_PASSES - 1,
+                    )
         for i in range(ROW_TILES):
             normed = work.tile([P, OUT_TILES, P], F32, name="hid%d_normed" % i)
             nc.scalar.activation(
@@ -227,14 +241,13 @@ def tile_layernormgrucell_pb_s_kernel(tc, x, h, c, W_u, U_u, ln_gamma, ln_beta, 
         step = [work.tile([P, H], F32, name="step%d" % i) for i in range(ROW_TILES)]
         result = [work.tile([P, H], F32, name="result%d" % i) for i in range(ROW_TILES)]
         out_tiles = out.rearrange("(p i) n -> i p n", i=ROW_TILES)
-        diff = [work.tile([P, H], F32, name="diff%d" % i) for i in range(ROW_TILES)]
-        nc.gpsimd.tensor_sub(out=diff[0][:], in0=c_rows[:, 0, :], in1=h_rows[:, 0, :])
         for i in range(ROW_TILES):
             nc.vector.bn_stats(out=stats[:, ROW_TILES + i, 0:6], in_=acc_x[i][:])
         for i in range(ROW_TILES):
             nc.vector.bn_aggr(out=x_mean_var[:, i, :], in_=stats[:, ROW_TILES + i, :])
         nc.gpsimd.tensor_tensor(out=x_rstd[:], in0=x_mean_var[:, :, 1], in1=neg_half[:], op=ALU.pow)
-        nc.gpsimd.tensor_sub(out=diff[1][:], in0=c_rows[:, 1, :], in1=h_rows[:, 1, :])
+        diff.append(work.tile([P, H], F32, name="diff1"))
+        nc.gpsimd.tensor_sub(out=diff[1][:], in0=c_rows[1][:], in1=h_rows[:, 1, :])
         for i in range(ROW_TILES):
             nc.vector.scalar_tensor_tensor(
                 out=centred[i][:], in0=acc_x[i][:], scalar=x_mean_var[:, i, 0:1], in1=gamma_x[:],

@@ -254,11 +254,12 @@ def tile_layernormgrucell_pb_s_kernel(tc, x, h, c, W_u, U_u, ln_gamma, ln_beta, 
                 op0=ALU.subtract, op1=ALU.mult,
             )
         for i in range(ROW_TILES):
-            nc.vector.scalar_tensor_tensor(
-                out=logit[i][:], in0=centred[i][:], scalar=x_rstd[:, i : i + 1], in1=hidden_part[i],
-                op0=ALU.mult, op1=ALU.add,
-            )
-            nc.scalar.activation(out=gate[i][:], in_=logit[i][:], func=ACT.Sigmoid)
+            for cols in (slice(0, H // 2), slice(H // 2, H)):
+                nc.vector.scalar_tensor_tensor(
+                    out=logit[i][:, cols], in0=centred[i][:, cols], scalar=x_rstd[:, i : i + 1],
+                    in1=hidden_part[i][:, cols], op0=ALU.mult, op1=ALU.add,
+                )
+                nc.scalar.activation(out=gate[i][:, cols], in_=logit[i][:, cols], func=ACT.Sigmoid)
         for i in range(ROW_TILES):
             nc.vector.tensor_mul(out=step[i][:], in0=gate[i][:], in1=diff[i][:])
         for i in range(ROW_TILES):

@@ -25,17 +25,21 @@ EPS = 1e-5
 FLOPS = 2 * B * H * (H + IN)
 
 
-def flip(nc, pools, ident, blocks, copy, name):
+def flip(nc, pools, ident, blocks, copy, name, interleave=False):
     n_blocks = len(blocks)
     flipped = pools["flipped"].tile([P, 2 * BLOCKS, P], F32, tag="flipped")
     for b in range(n_blocks):
         for u in range(2):
             nc.tensor.transpose(flipped[:, 2 * b + u, :], blocks[b][:, u * P : (u + 1) * P], ident[:])
     grouped = pools["stage"].tile([P, n_blocks * P * PACK], BF16, align_bytes=64, tag=name + "_grouped", name=name + "_grouped")
-    copy(
-        out=grouped[:].bitcast(F32).rearrange("p (b r u) -> p b r u", b=n_blocks, u=2),
-        in_=flipped[:, 0 : 2 * n_blocks, :].rearrange("p (b u) r -> p b r u", u=2),
-    )
+    planes = flipped[:, 0 : 2 * n_blocks, :]
+    if interleave:
+        in_rows = planes.rearrange("p (b u) r -> p r b u", u=2)
+        out_rows = grouped[:].bitcast(F32).rearrange("p (r b u) -> p r b u", b=n_blocks, u=2)
+    else:
+        in_rows = planes.rearrange("p (b u) r -> p b r u", u=2)
+        out_rows = grouped[:].bitcast(F32).rearrange("p (b r u) -> p b r u", b=n_blocks, u=2)
+    copy(out=out_rows, in_=in_rows)
     return grouped
 
 
@@ -119,11 +123,9 @@ def tile_layernormgrucell_pb_s_kernel(tc, x, h, c, W_u, U_u, ln_gamma, ln_beta, 
             w = rows.tile([P, BLOCKS, H], BF16, name="w%d" % n)
             nc.sync.dma_start(
                 out=w[:],
-                in_=W_u[n * BLOCKS * P : (n + 1) * BLOCKS * P, :].rearrange("(b p) k -> p b k", p=P),
+                in_=W_u[n * BLOCKS * P : (n + 1) * BLOCKS * P, :].rearrange("(p b) k -> p b k", p=P),
             )
             w_rows.append(w)
-        nc.sync.dma_start(out=vec_rows[0:8, 0, :], in_=ln_gamma.rearrange("l (q n) -> (l q) n", n=P))
-        nc.sync.dma_start(out=vec_rows[8:12, :, :], in_=ln_beta.rearrange("l (q n) -> q l n", n=P))
         u_rows = []
         x_rows = []
         x_tiles = x.rearrange("(p i) k -> i p k", i=ROW_TILES)
@@ -136,7 +138,10 @@ def tile_layernormgrucell_pb_s_kernel(tc, x, h, c, W_u, U_u, ln_gamma, ln_beta, 
             x_rows.append(rows.tile([P, IN], BF16, name="x%d" % i))
             nc.sync.dma_start(out=x_rows[i][:], in_=x_tiles[i])
 
-        for n in range(OUT_TILES - 1):
+        load_u(0)
+        nc.sync.dma_start(out=vec_rows[0:8, 0, :], in_=ln_gamma.rearrange("l (q n) -> (l q) n", n=P))
+        nc.sync.dma_start(out=vec_rows[8:12, :, :], in_=ln_beta.rearrange("l (q n) -> q l n", n=P))
+        for n in range(1, OUT_TILES - 1):
             load_u(n)
         load_x(0)
         load_u(OUT_TILES - 1)
@@ -150,19 +155,14 @@ def tile_layernormgrucell_pb_s_kernel(tc, x, h, c, W_u, U_u, ln_gamma, ln_beta, 
             quantise(nc, flip(nc, pools, ident, [h_rows[:, i, :].bitcast(F32)], on_scalar, "h%d" % i)[:], h_mx, i * P)
 
         vec_f32 = const.tile([P, P], F32)
-        nc.vector.tensor_add(out=vec_f32[:], in0=vec_rows[:, 0, :], in1=vec_rows[:, 1, :])
+        nc.gpsimd.tensor_add(out=vec_f32[:], in0=vec_rows[:, 0, :], in1=vec_rows[:, 1, :])
 
         w_mx = mx_tile(pools, H, "w")
         for n in range(W_UNITS):
             words = [w_rows[n][:, b, :].bitcast(F32) for b in range(BLOCKS)]
-            grouped = flip(nc, pools, ident, words, on_scalar, "w%d" % n)
+            grouped = flip(nc, pools, ident, words, on_scalar, "w%d" % n, True)
             quantise(nc, grouped[:], w_mx, n * BLOCKS * P)
             keep_busy(1)
-
-        vec_flipped = pools["flipped"].tile([P, OUT_TILES, P], F32, tag="flipped")
-        nc.tensor.transpose(vec_flipped[:, 0, :], vec_f32[:], ident[:])
-        vec_cols = const.tile([P, 3 * OUT_TILES], F32)
-        nc.scalar.copy(out=vec_cols[:], in_=vec_flipped[:, 0, 0 : 3 * OUT_TILES])
 
         u_mx = [mx_tile(pools, X_PASSES * P, "u%d" % n) for n in range(OUT_TILES)]
 
@@ -177,6 +177,10 @@ def tile_layernormgrucell_pb_s_kernel(tc, x, h, c, W_u, U_u, ln_gamma, ln_beta, 
         acc_h = [pools["acc"].tile([P, H], F32, tag="acc_h%d" % i, name="acc_h%d" % i) for i in range(ROW_TILES)]
         for i in range(ROW_TILES):
             mx_pass(nc, acc_h[i][:], h_mx, i, w_mx, slice(0, H), True, True)
+        vec_flipped = pools["flipped"].tile([P, OUT_TILES, P], F32, tag="flipped")
+        nc.tensor.transpose(vec_flipped[:, 0, :], vec_f32[:], ident[:])
+        vec_cols = const.tile([P, 3 * OUT_TILES], F32)
+        nc.scalar.copy(out=vec_cols[:], in_=vec_flipped[:, 0, 0 : 3 * OUT_TILES])
         mean_var = small.tile([P, ROW_TILES, 2], F32, name="hid_mean_var")
         rstd = small.tile([P, ROW_TILES], F32, name="hid_rstd")
         neg_mean = small.tile([P, ROW_TILES], F32, name="hid_neg_mean")

from contextlib import ExitStack

import concourse.mybir as mybir
from concourse.masks import make_identity

F32 = mybir.dt.float32
BF16 = mybir.dt.bfloat16
U32 = mybir.dt.uint32
U8 = mybir.dt.uint8
FP8X4 = mybir.dt.float8_e4m3fn_x4
ALU = mybir.AluOpType
ACT = mybir.ActivationFunctionType

P = 128
B, IN, H = 256, 1024, 512
PACK = 4
K_PASS = P * PACK
ROW_TILES = B // P
OUT_TILES = H // P
BLOCKS = 2
W_UNITS = H // (BLOCKS * P)
X_PASSES = IN // K_PASS
EPS = 1e-5

FLOPS = 2 * B * H * (H + IN)


def flip(nc, pools, ident, blocks, copy, name, interleave=False):
    n_blocks = len(blocks)
    flipped = pools["flipped"].tile([P, 2 * BLOCKS, P], F32, tag="flipped")
    for b in range(n_blocks):
        for u in range(2):
            nc.tensor.transpose(flipped[:, 2 * b + u, :], blocks[b][:, u * P : (u + 1) * P], ident[:])
    grouped = pools["stage"].tile([P, n_blocks * P * PACK], BF16, align_bytes=64, tag=name + "_grouped", name=name + "_grouped")
    planes = flipped[:, 0 : 2 * n_blocks, :]
    if interleave:
        in_rows = planes.rearrange("p (b u) r -> p r b u", u=2)
        out_rows = grouped[:].bitcast(F32).rearrange("p (r b u) -> p r b u", b=n_blocks, u=2)
    else:
        in_rows = planes.rearrange("p (b u) r -> p b r u", u=2)
        out_rows = grouped[:].bitcast(F32).rearrange("p (b r u) -> p b r u", b=n_blocks, u=2)
    copy(out=out_rows, in_=in_rows)
    return grouped


def mx_tile(pools, width, name):
    codes = pools["keep"].tile([P, width], U32, align_bytes=64, name=name + "_codes")
    scales = pools["keep"].tile([P, width], U8, align_bytes=64, name=name + "_scales")
    return codes, scales


def quantise(nc, grouped, mx, first):
    cols = slice(first, first + grouped.shape[-1] // PACK)
    nc.vector.quantize_mx(out=mx[0][:, cols].bitcast(FP8X4), scales=mx[1][:, cols], in_=grouped)


def mx_pass(nc, acc, acts, block, weights, outs, start, stop):
    cols = slice(block * P, (block + 1) * P)
    nc.tensor.matmul_mx(
        out=acc,
        lhsT=acts[0][:, cols].bitcast(FP8X4),
        lhsT_scale=acts[1][:, cols],
        rhs=weights[0][:, outs].bitcast(FP8X4),
        rhs_scale=weights[1][:, outs],
        start=start,
        stop=stop,
    )


def spread_vector(nc, pools, ident, vec_cols, v, name):
    spread_ps = pools["flipped"].tile([P, OUT_TILES, P], F32, tag="flipped")
    for q in range(OUT_TILES):
        col = v * OUT_TILES + q
        nc.tensor.transpose(spread_ps[:, q, :], vec_cols[:, col : col + 1].to_broadcast([P, P]), ident[:])
    spread = pools["const"].tile([P, H], F32, name=name)
    nc.scalar.copy(out=spread[:], in_=spread_ps[:].rearrange("p q n -> p (q n)"))
    return spread


def tile_layernormgrucell_pb_s_kernel(tc, x, h, c, W_u, U_u, ln_gamma, ln_beta, out):
    nc = tc.nc
    with ExitStack() as ctx:
        pools = {
            "const": ctx.enter_context(tc.tile_pool(name="const", bufs=1)),
            "rows": ctx.enter_context(tc.tile_pool(name="rows", bufs=1)),
            "stage": ctx.enter_context(tc.tile_pool(name="stage", bufs=1)),
            "keep": ctx.enter_context(tc.tile_pool(name="keep", bufs=1)),
            "small": ctx.enter_context(tc.tile_pool(name="small", bufs=1)),
            "work": ctx.enter_context(tc.tile_pool(name="work", bufs=1)),
            "flipped": ctx.enter_context(tc.psum_pool(name="flipped", bufs=4)),
            "acc": ctx.enter_context(tc.psum_pool(name="acc", bufs=1)),
        }
        const, rows, small, work = pools["const"], pools["rows"], pools["small"], pools["work"]
        ctx.enter_context(tc.manual_schedule())
        on_scalar, on_vector = nc.scalar.copy, nc.vector.tensor_copy

        zeros = const.tile([P, P], F32)
        nc.vector.memset(zeros[:], 0.0)
        ident = const.tile([P, P], F32)
        make_identity(nc, ident[:])
        vec_rows = const.tile([P, 2, P], BF16)
        nc.vector.memset(vec_rows[:], 0.0)
        neg_half = const.tile([P, ROW_TILES], F32)
        nc.vector.memset(neg_half[:], -0.5)
        idle_ps = pools["acc"].tile([P, P], F32, tag="acc_x0", name="idle_ps")

        def keep_busy(count):
            for rep in range(count):
                nc.tensor.matmul(out=idle_ps[:], lhsT=zeros[:], rhs=zeros[:], start=True, stop=True)

        keep_busy(3)
        stats = const.tile([P, 2 * ROW_TILES, 9], F32)
        nc.vector.memset(stats[:], 0.0)
        nc.vector.memset(stats[:, :, 8:9], H * EPS)
        warm = const.tile([P, 1], F32)
        nc.scalar.activation(out=warm[:], in_=neg_half[:, 0:1], func=ACT.Sigmoid)

        h_rows = rows.tile([P, ROW_TILES, H], BF16)
        for i in range(ROW_TILES):
            nc.sync.dma_start(out=h_rows[:, i, :], in_=h.rearrange("(p i) k -> i p k", i=ROW_TILES)[i])
        w_rows = []
        for n in range(W_UNITS):
            w = rows.tile([P, BLOCKS, H], BF16, name="w%d" % n)
            nc.sync.dma_start(
                out=w[:],
                in_=W_u[n * BLOCKS * P : (n + 1) * BLOCKS * P, :].rearrange("(p b) k -> p b k", p=P),
            )
            w_rows.append(w)
        u_rows = []
        x_rows = []
        x_tiles = x.rearrange("(p i) k -> i p k", i=ROW_TILES)

        def load_u(n):
            u_rows.append(rows.tile([P, IN], BF16, name="u%d" % n))
            nc.sync.dma_start(out=u_rows[n][:], in_=U_u[n * P : (n + 1) * P, :])

        def load_x(i):
            x_rows.append(rows.tile([P, IN], BF16, name="x%d" % i))
            nc.sync.dma_start(out=x_rows[i][:], in_=x_tiles[i])

        load_u(0)
        nc.sync.dma_start(out=vec_rows[0:8, 0, :], in_=ln_gamma.rearrange("l (q n) -> (l q) n", n=P))
        nc.sync.dma_start(out=vec_rows[8:12, :, :], in_=ln_beta.rearrange("l (q n) -> q l n", n=P))
        for n in range(1, OUT_TILES - 1):
            load_u(n)
        load_x(0)
        load_u(OUT_TILES - 1)
        load_x(1)
        c_rows = [rows.tile([P, H], BF16, name="c%d" % i) for i in range(ROW_TILES)]
        for i in range(ROW_TILES):
            nc.sync.dma_start(out=c_rows[i][:], in_=c.rearrange("(p i) k -> i p k", i=ROW_TILES)[i])

        h_mx = mx_tile(pools, ROW_TILES * P, "h")
        for i in range(ROW_TILES):
            quantise(nc, flip(nc, pools, ident, [h_rows[:, i, :].bitcast(F32)], on_scalar, "h%d" % i)[:], h_mx, i * P)

        vec_f32 = const.tile([P, P], F32)
        nc.gpsimd.tensor_add(out=vec_f32[:], in0=vec_rows[:, 0, :], in1=vec_rows[:, 1, :])

        w_mx = mx_tile(pools, H, "w")
        for n in range(W_UNITS):
            words = [w_rows[n][:, b, :].bitcast(F32) for b in range(BLOCKS)]
            grouped = flip(nc, pools, ident, words, on_scalar, "w%d" % n, True)
            quantise(nc, grouped[:], w_mx, n * BLOCKS * P)
            keep_busy(1)

        u_mx = [mx_tile(pools, X_PASSES * P, "u%d" % n) for n in range(OUT_TILES)]

        def flip_in(row_tile, copy, name):
            words = row_tile[:].bitcast(F32)
            return flip(nc, pools, ident, [words[:, g * 2 * P : (g + 1) * 2 * P] for g in range(X_PASSES)], copy, name)

        def quantise_u(n):
            quantise(nc, u_grouped[n][:], u_mx[n], 0)

        u_grouped = [flip_in(u_rows[n], on_scalar, "u%d" % n) for n in range(OUT_TILES - 1)]
        acc_h = [pools["acc"].tile([P, H], F32, tag="acc_h%d" % i, name="acc_h%d" % i) for i in range(ROW_TILES)]
        for i in range(ROW_TILES):
            mx_pass(nc, acc_h[i][:], h_mx, i, w_mx, slice(0, H), True, True)
        vec_flipped = pools["flipped"].tile([P, OUT_TILES, P], F32, tag="flipped")
        nc.tensor.transpose(vec_flipped[:, 0, :], vec_f32[:], ident[:])
        vec_cols = const.tile([P, 3 * OUT_TILES], F32)
        nc.scalar.copy(out=vec_cols[:], in_=vec_flipped[:, 0, 0 : 3 * OUT_TILES])
        mean_var = small.tile([P, ROW_TILES, 2], F32, name="hid_mean_var")
        rstd = small.tile([P, ROW_TILES], F32, name="hid_rstd")
        neg_mean = small.tile([P, ROW_TILES], F32, name="hid_neg_mean")
        shift = small.tile([P, ROW_TILES], F32, name="hid_shift")
        quantise_u(0)
        quantise_u(1)
        nc.vector.bn_stats(out=stats[:, 0, 0:6], in_=acc_h[0][:])
        nc.vector.bn_stats(out=stats[:, 1, 0:6], in_=acc_h[1][:])
        nc.vector.bn_aggr(out=mean_var[:, 0, :], in_=stats[:, 0, :])
        nc.vector.bn_aggr(out=mean_var[:, 1, :], in_=stats[:, 1, :])
        nc.vector.tensor_scalar_mul(neg_mean[:], mean_var[:, :, 0], -1.0)
        nc.gpsimd.tensor_tensor(out=rstd[:], in0=mean_var[:, :, 1], in1=neg_half[:], op=ALU.pow)
        nc.gpsimd.tensor_tensor(out=shift[:], in0=neg_mean[:], in1=rstd[:], op=ALU.mult)
        quantise_u(2)

        x_mx = [mx_tile(pools, X_PASSES * P, "x%d" % i) for i in range(ROW_TILES)]
        quantise(nc, flip_in(x_rows[0], on_scalar, "x0")[:], x_mx[0], 0)
        u_grouped.append(flip_in(u_rows[3], on_scalar, "u3"))
        quantise_u(3)
        quantise(nc, flip_in(x_rows[1], on_scalar, "x1")[:], x_mx[1], 0)
        diff = [pools["stage"].tile([P, H], F32, tag="x1_grouped", align_bytes=64, name="diff0")]
        nc.gpsimd.tensor_sub(out=diff[0][:], in0=c_rows[0][:], in1=h_rows[:, 0, :])

        gamma_x = spread_vector(nc, pools, ident, vec_cols, 1, "gamma_x")
        keep_busy(2)

        acc_x, turned_ps, hidden_part = [], [], []
        for i in range(ROW_TILES):
            acc_x.append(pools["acc"].tile([P, H], F32, tag="acc_x%d" % i, name="acc_x%d" % i))
            for n in range(OUT_TILES):
                for g in range(X_PASSES):
                    mx_pass(
                        nc, acc_x[i][:, n * P : (n + 1) * P], x_mx[i], g, u_mx[n], slice(g * P, (g + 1) * P),
                        g == 0, g == X_PASSES - 1,
                    )
        for i in range(ROW_TILES):
            normed = work.tile([P, OUT_TILES, P], F32, name="hid%d_normed" % i)
            nc.scalar.activation(
                out=normed[:].rearrange("p q n -> p (q n)"), in_=acc_h[i][:], func=ACT.Identity,
                scale=rstd[:, i : i + 1], bias=shift[:, i : i + 1],
            )
            turned_ps.append(pools["flipped"].tile([P, OUT_TILES, P], F32, tag="flipped", name="turned_ps%d" % i))
            for q in range(OUT_TILES):
                nc.tensor.transpose(turned_ps[i][:, q, :], normed[:, q, :], ident[:])
        for i in range(ROW_TILES):
            turned = work.tile([P, OUT_TILES, P], F32, name="hid%d_turned" % i)
            for q in range(OUT_TILES):
                nc.scalar.activation(
                    out=turned[:, q, :], in_=turned_ps[i][:, q, :], func=ACT.Identity,
                    scale=vec_cols[:, q : q + 1], bias=vec_cols[:, 2 * OUT_TILES + q : 2 * OUT_TILES + q + 1],
                )
            hidden = pools["acc"].tile([P, OUT_TILES, P], F32, tag="acc_h%d" % i, name="hidden%d" % i)
            for q in range(OUT_TILES):
                nc.tensor.transpose(hidden[:, q, :], turned[:, q, :], ident[:])
            hidden_part.append(hidden[:].rearrange("p q n -> p (q n)"))

        x_mean_var = small.tile([P, ROW_TILES, 2], F32, name="inp_mean_var")
        x_rstd = small.tile([P, ROW_TILES], F32, name="inp_rstd")
        centred = [work.tile([P, H], F32, name="centred%d" % i) for i in range(ROW_TILES)]
        logit = [work.tile([P, H], F32, name="logit%d" % i) for i in range(ROW_TILES)]
        gate = [work.tile([P, H], F32, name="gate%d" % i) for i in range(ROW_TILES)]
        step = [work.tile([P, H], F32, name="step%d" % i) for i in range(ROW_TILES)]
        result = [work.tile([P, H], F32, name="result%d" % i) for i in range(ROW_TILES)]
        out_tiles = out.rearrange("(p i) n -> i p n", i=ROW_TILES)
        for i in range(ROW_TILES):
            nc.vector.bn_stats(out=stats[:, ROW_TILES + i, 0:6], in_=acc_x[i][:])
        for i in range(ROW_TILES):
            nc.vector.bn_aggr(out=x_mean_var[:, i, :], in_=stats[:, ROW_TILES + i, :])
        nc.gpsimd.tensor_tensor(out=x_rstd[:], in0=x_mean_var[:, :, 1], in1=neg_half[:], op=ALU.pow)
        diff.append(work.tile([P, H], F32, name="diff1"))
        nc.gpsimd.tensor_sub(out=diff[1][:], in0=c_rows[1][:], in1=h_rows[:, 1, :])
        for i in range(ROW_TILES):
            nc.vector.scalar_tensor_tensor(
                out=centred[i][:], in0=acc_x[i][:], scalar=x_mean_var[:, i, 0:1], in1=gamma_x[:],
                op0=ALU.subtract, op1=ALU.mult,
            )
        for i in range(ROW_TILES):
            for cols in (slice(0, H // 2), slice(H // 2, H)):
                nc.vector.scalar_tensor_tensor(
                    out=logit[i][:, cols], in0=centred[i][:, cols], scalar=x_rstd[:, i : i + 1],
                    in1=hidden_part[i][:, cols], op0=ALU.mult, op1=ALU.add,
                )
                nc.scalar.activation(out=gate[i][:, cols], in_=logit[i][:, cols], func=ACT.Sigmoid)
        for i in range(ROW_TILES):
            nc.vector.tensor_mul(out=step[i][:], in0=gate[i][:], in1=diff[i][:])
        for i in range(ROW_TILES):
            nc.vector.tensor_add(out=result[i][:], in0=step[i][:], in1=h_rows[:, i, :])
            nc.sync.dma_start(out=out_tiles[i], in_=result[i][:])
